import numpy as np
import ml_dtypes


def mxq(x, axis, fmt="e4m3"):
    dtype, down = {"e4m3": (ml_dtypes.float8_e4m3fn, 7), "e5m2": (ml_dtypes.float8_e5m2, 14)}[fmt]
    v = np.moveaxis(np.asarray(x, np.float32).astype(ml_dtypes.bfloat16).astype(np.float64), axis, -1)
    blocks = v.reshape(v.shape[:-1] + (-1, 32))
    amax = np.abs(blocks).max(-1, keepdims=True)
    byte = np.maximum(np.where(amax > 0, np.frexp(amax)[1] - 1 + 127, 0) - down, 1)
    scale = np.exp2(byte - 127.0)
    codes = (blocks / scale).astype(np.float32).astype(dtype).astype(np.float64)
    return np.moveaxis((codes * scale).reshape(v.shape), -1, axis)


WIDE = False


def mx_kscale(k):
    if not WIDE:
        return np.ones(k)
    levels = np.array([10, -10, 5, -5, 0])
    if k % 512:
        return np.exp2(np.random.permutation(np.resize(levels, k // 32))).repeat(32)
    a = np.empty((k // 512, 16))
    for p in range(k // 512):
        a[p, :8] = np.random.permutation(np.resize(levels, 8))
        for g in range(8):
            far = levels[np.abs(levels - a[p, g]) >= 10]
            a[p, g + 8] = far[np.random.randint(len(far))]
    return np.exp2(a.ravel()).repeat(32)


BF16 = ml_dtypes.bfloat16


def bf(x):
    return np.asarray(x, np.float32).astype(BF16)


def f64(x):
    return np.asarray(x).astype(np.float64)


E2M1 = np.array([0.0, 0.5, 1.0, 1.5, 2.0, 3.0, 4.0, 6.0, -0.0, -0.5, -1.0, -1.5, -2.0, -3.0, -4.0, -6.0])


def pack_weight(w, fmt):
    k, n = w.shape
    w = f64(bf(w)).reshape(k // 32, 32, n)
    amax = np.abs(w).max(1)
    if fmt == "e4m3":
        byte = np.frexp(amax)[1] - 1 + 127 - 7
    else:
        mant, ex = np.frexp(amax / 6.0)
        byte = np.where(mant > 0.5, ex, ex - 1) + 127
    byte = np.clip(np.where(amax > 0, byte, 1), 1, 254)
    scaled = (w * np.exp2(127.0 - byte)[:, None, :]).reshape(k, n).astype(np.float32)
    by_word = np.ascontiguousarray(scaled.reshape(k // 512, 128, 4, n).transpose(0, 1, 3, 2))
    if fmt == "e4m3":
        words = by_word.astype(ml_dtypes.float8_e4m3fn).view(np.uint8)
    else:
        c = by_word.astype(ml_dtypes.float4_e2m1fn).view(np.uint8) & 0xF
        words = c[..., 0::2] | (c[..., 1::2] << 4)
    return np.ascontiguousarray(words), np.ascontiguousarray(byte.astype(np.uint8).reshape(k // 512, 16, n))


def unpack_weight(words, scales, fmt):
    g, p, n, _ = words.shape
    if fmt == "e4m3":
        vals = np.ascontiguousarray(words).view(ml_dtypes.float8_e4m3fn).astype(np.float64)
    else:
        nib = np.empty((g, p, n, 4), np.uint8)
        nib[..., 0::2] = words & 0xF
        nib[..., 1::2] = words >> 4
        vals = E2M1[nib]
    vals = vals * np.repeat(np.exp2(scales.astype(np.float64) - 127.0), 8, axis=1)[..., None]
    return vals.transpose(0, 1, 3, 2).reshape(g * 512, n)


N, C, T, V, IC = 1, 4096, 2, 128, 2048
G = (IC * T) ** 0.25


def setup_inputs():
    s = mx_kscale(C)
    u = mx_kscale(IC * T)[::T]
    x = bf(np.random.standard_normal((N, C, T, V)) * s[None, :, None, None])
    Wa = np.random.standard_normal((IC, C)) * G / np.sqrt(C) / s[None, :] * u[:, None]
    Wa_words, Wa_scales = pack_weight(Wa.T, "e4m3")
    ba = bf(np.random.standard_normal(IC) * 0.3 * G * u)
    Wb = np.random.standard_normal((IC, C)) * G / np.sqrt(C) / s[None, :] / u[:, None]
    Wb_words, Wb_scales = pack_weight(Wb.T, "e4m3")
    bb = bf(np.random.standard_normal(IC) * 0.3 * G / u)
    A = bf(np.eye(V)[None] + 0.1 * np.random.standard_normal((1, V, V)))
    alpha = bf(2.0 + 0.2 * np.random.standard_normal(1))
    return {"x": x,
            "Wa_words": Wa_words,
            "Wa_scales": Wa_scales,
            "ba": ba,
            "Wb_words": Wb_words,
            "Wb_scales": Wb_scales,
            "bb": bb,
            "A": A,
            "alpha": alpha}


def reference(x, Wa_words, Wa_scales, ba, Wb_words, Wb_scales, bb, A, alpha):
    n, c, t, v = x.shape
    wa = unpack_weight(Wa_words, Wa_scales, "e4m3").T
    wb = unpack_weight(Wb_words, Wb_scales, "e4m3").T
    ic = wa.shape[0]
    xq = mxq(f64(x), 1, "e4m3").reshape(n, c, t * v)
    qa = (wa @ xq).reshape(n, ic, t, v) + f64(ba)[None, :, None, None]
    kb = (wb @ xq).reshape(n, ic, t, v) + f64(bb)[None, :, None, None]
    Q = qa.transpose(0, 3, 1, 2).reshape(n, v, ic * t)
    K = kb.reshape(n, ic * t, v)
    Graph_B = np.tanh((mxq(Q, 2, "e4m3") @ mxq(K, 1, "e4m3")) / (ic * t))
    z = f64(A) + Graph_B * f64(alpha)
    e = np.exp(z - z.max(-1, keepdims=True))
    return e / e.sum(-1, keepdims=True)

@@ -1,0 +1,266 @@
+from contextlib import ExitStack
+
+import concourse.masks as masks
+import concourse.mybir as mybir
+
+F32 = mybir.dt.float32
+BF16 = mybir.dt.bfloat16
+I32 = mybir.dt.int32
+U8 = mybir.dt.uint8
+FP8X4 = mybir.dt.float8_e4m3fn_x4
+ACT = mybir.ActivationFunctionType
+ALU = mybir.AluOpType
+AX = mybir.AxisListType
+
+P = 128
+C = 4096
+IC = 2048
+T = 2
+V = 128
+TV = T * V
+GROUPS = C // 512
+FLOPS = 2 * 2 * IC * C * TV + 2 * V * V * IC * T
+
+WHOLE = [(g, 0, 8) for g in range(GROUPS)]
+PIECES = [WHOLE, WHOLE, WHOLE, WHOLE[:6] + [(6, 0, 4), (7, 0, 4), (6, 4, 4), (7, 4, 2), (7, 6, 2)]]
+
+
+def tile_adaptivegraphconstruction_w_kernel(
+    tc, x, Wa_words, Wa_scales, ba, Wb_words, Wb_scales, bb, A, alpha, out
+):
+    nc = tc.nc
+    words = (Wa_words, Wb_words)
+    scales = (Wa_scales, Wb_scales)
+    with ExitStack() as ctx:
+        keep = ctx.enter_context(tc.tile_pool(name="keep", bufs=1))
+        psum = ctx.enter_context(tc.psum_pool(name="psum", bufs=1))
+        ctx.enter_context(tc.manual_schedule())
+
+        raw_pool = ctx.enter_context(tc.tile_pool(name="raw", bufs=10))
+        w_pool = ctx.enter_context(tc.tile_pool(name="w", bufs=8))
+        stage = keep.tile([P, 256], BF16, name="stage")
+        stage_p = keep.tile([P, 256], BF16, name="stage_p")
+        ident = keep.tile([P, P], BF16, name="ident")
+        bias = keep.tile([P, 32], F32, name="bias")
+        planes_raw = [keep.tile([P, IC], U8, name="planes_raw%d" % b, align_bytes=64) for b in range(4)]
+        a_sb = keep.tile([P, V], BF16, name="a_sb")
+        alpha_bf = keep.tile([P, 1], BF16, name="alpha_bf")
+        alpha_f = keep.tile([P, 1], F32, name="alpha_f")
+        warm_in = keep.tile([P, 1], F32, name="warm_in")
+        warm_out = keep.tile([P, 1], F32, name="warm_out")
+        planes = [keep.tile([P, IC], U8, name="planes%d" % b, align_bytes=64) for b in range(4)]
+        x_raw = [keep.tile([P, 4 * TV], BF16, name="x_raw%d" % g) for g in range(GROUPS)]
+        x_grp = [keep.tile([P, 4 * TV], BF16, name="x_grp%d" % g, align_bytes=64) for g in range(GROUPS)]
+        x_codes = [keep.tile([P, TV], I32, name="x_codes%d" % g, align_bytes=64) for g in range(GROUPS)]
+        x_scales = [keep.tile([P, TV], U8, name="x_scales%d" % g, align_bytes=64) for g in range(GROUPS)]
+        w = {}
+        q_grp = [keep.tile([P, 2048], BF16, name="q_grp%d" % ph, align_bytes=64) for ph in range(4)]
+        q_codes = [keep.tile([P, 512], I32, name="q_codes%d" % ph, align_bytes=64) for ph in range(4)]
+        q_scales = [keep.tile([P, 512], U8, name="q_scales%d" % ph, align_bytes=64) for ph in range(4)]
+
+        nc.vector.memset(planes_raw[0][:].bitcast(I32), 0)
+        nc.vector.memset(stage[:], 0.0)
+        nc.vector.memset(warm_in[:], 0.0)
+        for b in range(1, 4):
+            nc.vector.memset(planes_raw[b][:].bitcast(I32), 0)
+        masks.make_identity(nc, ident[:])
+        nc.scalar.dma_start(out=stage[0:8, :], in_=ba.rearrange("(i c) -> i c", c=256))
+        nc.scalar.dma_start(out=stage[8:16, :], in_=bb.rearrange("(i c) -> i c", c=256))
+        nc.scalar.dma_start(out=a_sb[:], in_=A[0])
+        nc.scalar.dma_start(out=alpha_bf[:], in_=alpha.partition_broadcast(P))
+        nc.scalar.activation(out=warm_out[:], in_=warm_in[:], func=ACT.Tanh)
+
+        xv = x.rearrange("n (g p j) t v -> (n g) p (j t v)", p=P, j=4)
+
+        def load_x(g):
+            nc.sync.dma_start(out=x_raw[g][:], in_=xv[g])
+
+        w_raw = {}
+
+        def load_w(ph, i):
+            wsel, half = divmod(ph, 2)
+            g, i0, n = PIECES[ph][i]
+            first = 4096 * half + 512 * i0
+            src = words[wsel][g].rearrange("p n t -> p (n t)")[:, first : first + 512 * n]
+            raw = raw_pool.tile([P, 1024], I32, name="raw", align_bytes=64)
+            w_raw[ph, i] = raw
+            nc.sync.dma_start(out=raw[:, 0 : 128 * n], in_=src.bitcast(I32))
+
+        def load_scales(wsel, b):
+            for quad in (0, 2, 1, 3):
+                nc.sync.dma_start(
+                    out=planes_raw[2 * wsel + b][32 * quad : 32 * quad + 16, :].bitcast(I32),
+                    in_=scales[wsel][4 * b : 4 * b + 4, 4 * quad : 4 * quad + 4, :].bitcast(I32),
+                )
+
+        load_x(0)
+        load_scales(0, 0)
+        for g in range(1, GROUPS):
+            load_x(g)
+
+        split = "p (b h r) -> p h b r"
+        nc.vector.tensor_copy(
+            out=stage_p[:].rearrange("p (h b r) -> p h b r", h=2, r=8),
+            in_=stage[:].rearrange(split, h=2, r=8),
+        )
+        bt_ps = psum.tile([P, 256], BF16, tag="bank7", name="bt_ps")
+        for h in range(2):
+            nc.tensor.transpose(bt_ps[:, 128 * h : 128 * (h + 1)], stage_p[:, 128 * h : 128 * (h + 1)], ident[:])
+
+        def regroup_x(g):
+            nc.vector.tensor_copy(
+                out=x_grp[g][:].rearrange("p (c i t) -> p c t i", i=4, t=4),
+                in_=x_raw[g][:].rearrange("p (t c i) -> p c t i", t=4, i=4),
+            )
+
+        def quantise_x(g):
+            nc.vector.quantize_mx(out=x_codes[g][:].bitcast(FP8X4), scales=x_scales[g][:], in_=x_grp[g][:])
+
+        regroup_x(0)
+        for g in range(1, GROUPS):
+            regroup_x(g)
+            quantise_x(g - 1)
+        quantise_x(GROUPS - 1)
+        for h in range(2):
+            nc.vector.tensor_copy(out=bias[:, 16 * h : 16 * (h + 1)], in_=bt_ps[:, 128 * h : 128 * h + 16])
+        nc.vector.tensor_copy(out=alpha_f[:], in_=alpha_bf[:])
+
+        def evacuate(ph, banks, j, on_vector=None):
+            wsel, half = divmod(ph, 2)
+            grp = q_grp[ph][:].rearrange("p (j v c) -> p j v c", j=4, c=4)
+            for u in range(2):
+                i = 2 * j + u
+                src = banks[i][:].rearrange("p (t v) -> p v t", t=T)
+                dst = grp[:, j, :, 2 * u : 2 * u + 2]
+                col = 16 * u + 8 * wsel + 4 * half + j
+                if (j % 2 == 0) if on_vector is None else on_vector:
+                    nc.vector.tensor_scalar(
+                        out=dst, in0=src, scalar1=bias[:, col : col + 1], scalar2=None, op0=ALU.add
+                    )
+                else:
+                    nc.scalar.activation(
+                        out=dst, in_=src, func=ACT.Identity, bias=bias[:, col : col + 1], scale=1.0
+                    )
+
+        def quantise_q(ph, j0, j1):
+            nc.vector.quantize_mx(
+                out=q_codes[ph][:, 128 * j0 : 128 * j1].bitcast(FP8X4),
+                scales=q_scales[ph][:, 128 * j0 : 128 * j1],
+                in_=q_grp[ph][:, 512 * j0 : 512 * j1],
+            )
+
+        def permute_scales(b):
+            nc.vector.tensor_copy(
+                out=planes[b][:].bitcast(I32).rearrange("p (h b r) -> p h b r", h=2, r=2),
+                in_=planes_raw[b][:].bitcast(I32).rearrange(split, h=2, r=2),
+            )
+
+        def permute_w(ph, i):
+            n = PIECES[ph][i][2]
+            tile = w_pool.tile([P, 1024], I32, name="w", align_bytes=64)
+            w[ph, i] = tile
+            nc.vector.tensor_copy(
+                out=tile[:, 0 : 128 * n].rearrange("p (h b r) -> p h b r", h=2, r=8),
+                in_=w_raw[ph, i][:, 0 : 128 * n].rearrange(split, h=2, r=8),
+            )
+
+        def passes(ph, piece, banks):
+            wsel, half = divmod(ph, 2)
+            g, i0, n = PIECES[ph][piece]
+            blk = planes[2 * wsel + g // 4]
+            k = 4 * (g % 4)
+            for i in range(i0, i0 + n):
+                j, u = divmod(i, 2)
+                col = 1024 * u + 512 * half + 128 * j
+                at = 64 * n * u + 128 * (j - i0 // 2)
+                nc.tensor.matmul_mx(
+                    out=banks[i][:],
+                    lhsT=w[ph, piece][:, at : at + 128].bitcast(FP8X4),
+                    lhsT_scale=blk[k:P, col : col + 128],
+                    rhs=x_codes[g][:].bitcast(FP8X4),
+                    rhs_scale=x_scales[g][:],
+                    start=(g == 0),
+                    stop=(g == GROUPS - 1),
+                )
+
+        def second(g_ps, n):
+            half, j = divmod(n, 4)
+            cols = slice(128 * j, 128 * (j + 1))
+            nc.tensor.matmul_mx(
+                out=g_ps[:],
+                lhsT=q_codes[half][:, cols].bitcast(FP8X4),
+                lhsT_scale=q_scales[half][:, cols],
+                rhs=q_codes[2 + half][:, cols].bitcast(FP8X4),
+                rhs_scale=q_scales[2 + half][:, cols],
+                start=(n == 0),
+                stop=(n == 7),
+            )
+
+        order = [(ph, i) for ph in range(4) for i in range(len(PIECES[ph]))]
+        state = {"loaded": 0, "permuted": 0}
+
+        def advance(ph, i):
+            now = order.index((ph, i))
+            while state["loaded"] < min(now + 9, len(order)):
+                p2, i2 = order[state["loaded"]]
+                if (p2, i2) == (0, 4):
+                    load_scales(0, 1)
+                if p2 == 2 and i2 % 4 == 0:
+                    load_scales(1, i2 // 4)
+                load_w(p2, i2)
+                state["loaded"] += 1
+            lead = 4 if now < len(order) - 4 else 2
+            while state["permuted"] < min(now + lead, len(order)):
+                p2, i2 = order[state["permuted"]]
+                if p2 % 2 == 0 and i2 % 4 == 0:
+                    permute_scales(p2 + i2 // 4)
+                permute_w(p2, i2)
+                state["permuted"] += 1
+
+        for ph in range(3):
+            banks = [psum.tile([P, TV], F32, tag="bank%d" % i, name="acc%d_%d" % (ph, i)) for i in range(8)]
+            for g in range(GROUPS):
+                advance(ph, g)
+                passes(ph, g, banks)
+            for j in range(4):
+                evacuate(ph, banks, j)
+            quantise_q(ph, 0, 4)
+
+        banks = [psum.tile([P, TV], F32, tag="bank%d" % i, name="acc3_%d" % i) for i in range(8)]
+        for piece in range(8):
+            advance(3, piece)
+            passes(3, piece, banks)
+        evacuate(3, banks, 0)
+        evacuate(3, banks, 1)
+        quantise_q(3, 0, 2)
+        advance(3, 8)
+        passes(3, 8, banks)
+        g_ps = psum.tile([P, V], F32, tag="bank0", name="g_ps")
+        for n in range(4):
+            second(g_ps, n)
+        advance(3, 9)
+        passes(3, 9, banks)
+        evacuate(3, banks, 2, False)
+        advance(3, 10)
+        passes(3, 10, banks)
+        evacuate(3, banks, 3, True)
+        quantise_q(3, 2, 4)
+        for n in range(4, 8):
+            second(g_ps, n)
+
+        th = keep.tile([P, V], F32, name="th")
+        z = keep.tile([P, V], F32, name="z")
+        e = keep.tile([P, V], F32, name="e")
+        res = keep.tile([P, V], F32, name="res")
+        negmax = keep.tile([P, 1], F32, name="negmax")
+        total = keep.tile([P, 1], F32, name="total")
+        recip = keep.tile([P, 1], F32, name="recip")
+        nc.scalar.activation(out=th[:], in_=g_ps[:], func=ACT.Tanh, scale=1.0 / (IC * T))
+        nc.vector.scalar_tensor_tensor(
+            out=z[:], in0=th[:], scalar=alpha_f[:, 0:1], in1=a_sb[:], op0=ALU.mult, op1=ALU.add
+        )
+        nc.vector.tensor_reduce(out=negmax[:], in_=z[:], axis=AX.X, op=ALU.max, negate=True)
+        nc.scalar.activation(out=e[:], in_=z[:], func=ACT.Exp, bias=negmax[:, 0:1], scale=1.0, accum_out=total[:])
+        nc.vector.reciprocal(out=recip[:], in_=total[:])
+        nc.vector.tensor_scalar(out=res[:], in0=e[:], scalar1=recip[:, 0:1], scalar2=None, op0=ALU.mult)
+        nc.sync.dma_start(out=out[0], in_=res[:])

@@ -21,8 +21,9 @@ TV = T * V
 GROUPS = C // 512
 FLOPS = 2 * 2 * IC * C * TV + 2 * V * V * IC * T
 
-WHOLE = [(g, 0, 8) for g in range(GROUPS)]
-PIECES = [WHOLE, WHOLE, WHOLE, WHOLE[:6] + [(6, 0, 4), (7, 0, 4), (6, 4, 4), (7, 4, 2), (7, 6, 2)]]
+WHOLE = [(g, 0, 4) for g in range(GROUPS)]
+PIECES = [WHOLE, WHOLE, WHOLE, WHOLE[:6] + [(6, 0, 2), (7, 0, 2), (6, 2, 2), (7, 2, 1), (7, 3, 1)]]
+ORDER = [(ph, i) for ph in range(4) for i in range(len(PIECES[ph]))]
 
 
 def tile_adaptivegraphconstruction_w_kernel(
@@ -33,58 +34,45 @@ def tile_adaptivegraphconstruction_w_kernel(
     scales = (Wa_scales, Wb_scales)
     with ExitStack() as ctx:
         keep = ctx.enter_context(tc.tile_pool(name="keep", bufs=1))
+        raw_pool = ctx.enter_context(tc.tile_pool(name="raw", bufs=10))
+        w_pool = ctx.enter_context(tc.tile_pool(name="w", bufs=8))
         psum = ctx.enter_context(tc.psum_pool(name="psum", bufs=1))
         ctx.enter_context(tc.manual_schedule())
 
-        raw_pool = ctx.enter_context(tc.tile_pool(name="raw", bufs=10))
-        w_pool = ctx.enter_context(tc.tile_pool(name="w", bufs=8))
         stage = keep.tile([P, 256], BF16, name="stage")
         stage_p = keep.tile([P, 256], BF16, name="stage_p")
         ident = keep.tile([P, P], BF16, name="ident")
         bias = keep.tile([P, 32], F32, name="bias")
-        planes_raw = [keep.tile([P, IC], U8, name="planes_raw%d" % b, align_bytes=64) for b in range(4)]
         a_sb = keep.tile([P, V], BF16, name="a_sb")
         alpha_bf = keep.tile([P, 1], BF16, name="alpha_bf")
         alpha_f = keep.tile([P, 1], F32, name="alpha_f")
         warm_in = keep.tile([P, 1], F32, name="warm_in")
         warm_out = keep.tile([P, 1], F32, name="warm_out")
+        planes_raw = [keep.tile([P, IC], U8, name="planes_raw%d" % b, align_bytes=64) for b in range(4)]
         planes = [keep.tile([P, IC], U8, name="planes%d" % b, align_bytes=64) for b in range(4)]
         x_raw = [keep.tile([P, 4 * TV], BF16, name="x_raw%d" % g) for g in range(GROUPS)]
         x_grp = [keep.tile([P, 4 * TV], BF16, name="x_grp%d" % g, align_bytes=64) for g in range(GROUPS)]
         x_codes = [keep.tile([P, TV], I32, name="x_codes%d" % g, align_bytes=64) for g in range(GROUPS)]
         x_scales = [keep.tile([P, TV], U8, name="x_scales%d" % g, align_bytes=64) for g in range(GROUPS)]
-        w = {}
         q_grp = [keep.tile([P, 2048], BF16, name="q_grp%d" % ph, align_bytes=64) for ph in range(4)]
         q_codes = [keep.tile([P, 512], I32, name="q_codes%d" % ph, align_bytes=64) for ph in range(4)]
         q_scales = [keep.tile([P, 512], U8, name="q_scales%d" % ph, align_bytes=64) for ph in range(4)]
-
-        nc.vector.memset(planes_raw[0][:].bitcast(I32), 0)
-        nc.vector.memset(stage[:], 0.0)
-        nc.vector.memset(warm_in[:], 0.0)
-        for b in range(1, 4):
-            nc.vector.memset(planes_raw[b][:].bitcast(I32), 0)
-        masks.make_identity(nc, ident[:])
-        nc.scalar.dma_start(out=stage[0:8, :], in_=ba.rearrange("(i c) -> i c", c=256))
-        nc.scalar.dma_start(out=stage[8:16, :], in_=bb.rearrange("(i c) -> i c", c=256))
-        nc.scalar.dma_start(out=a_sb[:], in_=A[0])
-        nc.scalar.dma_start(out=alpha_bf[:], in_=alpha.partition_broadcast(P))
-        nc.scalar.activation(out=warm_out[:], in_=warm_in[:], func=ACT.Tanh)
+        w_raw = {}
+        w = {}
 
         xv = x.rearrange("n (g p j) t v -> (n g) p (j t v)", p=P, j=4)
 
         def load_x(g):
             nc.sync.dma_start(out=x_raw[g][:], in_=xv[g])
 
-        w_raw = {}
-
         def load_w(ph, i):
             wsel, half = divmod(ph, 2)
-            g, i0, n = PIECES[ph][i]
-            first = 4096 * half + 512 * i0
-            src = words[wsel][g].rearrange("p n t -> p (n t)")[:, first : first + 512 * n]
+            g, j0, n = PIECES[ph][i]
+            first = 4096 * half + 1024 * j0
+            src = words[wsel][g].rearrange("p n t -> p (n t)")[:, first : first + 1024 * n]
             raw = raw_pool.tile([P, 1024], I32, name="raw", align_bytes=64)
             w_raw[ph, i] = raw
-            nc.sync.dma_start(out=raw[:, 0 : 128 * n], in_=src.bitcast(I32))
+            nc.sync.dma_start(out=raw[:, 0 : 256 * n], in_=src.bitcast(I32))
 
         def load_scales(wsel, b):
             for quad in (0, 2, 1, 3):
@@ -93,65 +81,12 @@ def tile_adaptivegraphconstruction_w_kernel(
                     in_=scales[wsel][4 * b : 4 * b + 4, 4 * quad : 4 * quad + 4, :].bitcast(I32),
                 )
 
-        load_x(0)
-        load_scales(0, 0)
-        for g in range(1, GROUPS):
-            load_x(g)
-
         split = "p (b h r) -> p h b r"
-        nc.vector.tensor_copy(
-            out=stage_p[:].rearrange("p (h b r) -> p h b r", h=2, r=8),
-            in_=stage[:].rearrange(split, h=2, r=8),
-        )
-        bt_ps = psum.tile([P, 256], BF16, tag="bank7", name="bt_ps")
-        for h in range(2):
-            nc.tensor.transpose(bt_ps[:, 128 * h : 128 * (h + 1)], stage_p[:, 128 * h : 128 * (h + 1)], ident[:])
-
-        def regroup_x(g):
-            nc.vector.tensor_copy(
-                out=x_grp[g][:].rearrange("p (c i t) -> p c t i", i=4, t=4),
-                in_=x_raw[g][:].rearrange("p (t c i) -> p c t i", t=4, i=4),
-            )
-
-        def quantise_x(g):
-            nc.vector.quantize_mx(out=x_codes[g][:].bitcast(FP8X4), scales=x_scales[g][:], in_=x_grp[g][:])
-
-        regroup_x(0)
-        for g in range(1, GROUPS):
-            regroup_x(g)
-            quantise_x(g - 1)
-        quantise_x(GROUPS - 1)
-        for h in range(2):
-            nc.vector.tensor_copy(out=bias[:, 16 * h : 16 * (h + 1)], in_=bt_ps[:, 128 * h : 128 * h + 16])
-        nc.vector.tensor_copy(out=alpha_f[:], in_=alpha_bf[:])
-
-        def evacuate(ph, banks, j, on_vector=None):
-            wsel, half = divmod(ph, 2)
-            grp = q_grp[ph][:].rearrange("p (j v c) -> p j v c", j=4, c=4)
-            for u in range(2):
-                i = 2 * j + u
-                src = banks[i][:].rearrange("p (t v) -> p v t", t=T)
-                dst = grp[:, j, :, 2 * u : 2 * u + 2]
-                col = 16 * u + 8 * wsel + 4 * half + j
-                if (j % 2 == 0) if on_vector is None else on_vector:
-                    nc.vector.tensor_scalar(
-                        out=dst, in0=src, scalar1=bias[:, col : col + 1], scalar2=None, op0=ALU.add
-                    )
-                else:
-                    nc.scalar.activation(
-                        out=dst, in_=src, func=ACT.Identity, bias=bias[:, col : col + 1], scale=1.0
-                    )
-
-        def quantise_q(ph, j0, j1):
-            nc.vector.quantize_mx(
-                out=q_codes[ph][:, 128 * j0 : 128 * j1].bitcast(FP8X4),
-                scales=q_scales[ph][:, 128 * j0 : 128 * j1],
-                in_=q_grp[ph][:, 512 * j0 : 512 * j1],
-            )
+        joined = "p (h b r) -> p h b r"
 
         def permute_scales(b):
             nc.vector.tensor_copy(
-                out=planes[b][:].bitcast(I32).rearrange("p (h b r) -> p h b r", h=2, r=2),
+                out=planes[b][:].bitcast(I32).rearrange(joined, h=2, r=2),
                 in_=planes_raw[b][:].bitcast(I32).rearrange(split, h=2, r=2),
             )
 
@@ -160,28 +95,58 @@ def tile_adaptivegraphconstruction_w_kernel(
             tile = w_pool.tile([P, 1024], I32, name="w", align_bytes=64)
             w[ph, i] = tile
             nc.vector.tensor_copy(
-                out=tile[:, 0 : 128 * n].rearrange("p (h b r) -> p h b r", h=2, r=8),
-                in_=w_raw[ph, i][:, 0 : 128 * n].rearrange(split, h=2, r=8),
+                out=tile[:, 0 : 256 * n].rearrange(joined, h=2, r=8),
+                in_=w_raw[ph, i][:, 0 : 256 * n].rearrange(split, h=2, r=8),
             )
 
-        def passes(ph, piece, banks):
+        def regroup_x(g):
+            dst = x_grp[g][:].rearrange("p (c i t) -> p c t i", i=4, t=4)
+            src = x_raw[g][:].rearrange("p (t c i) -> p c t i", t=4, i=4)
+            if g == 0:
+                nc.vector.tensor_copy(out=dst, in_=src)
+            else:
+                nc.scalar.copy(out=dst, in_=src)
+
+        def quantise_x(g):
+            nc.vector.quantize_mx(out=x_codes[g][:].bitcast(FP8X4), scales=x_scales[g][:], in_=x_grp[g][:])
+
+        def passes(ph, i, acc):
             wsel, half = divmod(ph, 2)
-            g, i0, n = PIECES[ph][piece]
+            g, j0, n = PIECES[ph][i]
             blk = planes[2 * wsel + g // 4]
             k = 4 * (g % 4)
-            for i in range(i0, i0 + n):
-                j, u = divmod(i, 2)
-                col = 1024 * u + 512 * half + 128 * j
-                at = 64 * n * u + 128 * (j - i0 // 2)
-                nc.tensor.matmul_mx(
-                    out=banks[i][:],
-                    lhsT=w[ph, piece][:, at : at + 128].bitcast(FP8X4),
-                    lhsT_scale=blk[k:P, col : col + 128],
-                    rhs=x_codes[g][:].bitcast(FP8X4),
-                    rhs_scale=x_scales[g][:],
-                    start=(g == 0),
-                    stop=(g == GROUPS - 1),
+            for j in range(j0, j0 + n):
+                for u in range(2):
+                    col = 1024 * u + 512 * half + 128 * j
+                    at = 128 * n * u + 128 * (j - j0)
+                    nc.tensor.matmul_mx(
+                        out=acc[j][u],
+                        lhsT=w[ph, i][:, at : at + 128].bitcast(FP8X4),
+                        lhsT_scale=blk[k:P, col : col + 128],
+                        rhs=x_codes[g][:].bitcast(FP8X4),
+                        rhs_scale=x_scales[g][:],
+                        start=(g == 0 and (u == 0 or acc[j][2])),
+                        stop=(g == GROUPS - 1 and (u == 1 or acc[j][2])),
+                    )
+
+        def evacuate(ph, acc, j, u, on_vector):
+            wsel, half = divmod(ph, 2)
+            src = acc[j][u].rearrange("p (t v) -> p v t", t=T)
+            dst = q_grp[ph][:].rearrange("p (j v c) -> p j v c", j=4, c=4)[:, j, :, 2 * u : 2 * u + 2]
+            col = 16 * u + 8 * wsel + 4 * half + j
+            if on_vector:
+                nc.vector.tensor_scalar(
+                    out=dst, in0=src, scalar1=bias[:, col : col + 1], scalar2=None, op0=ALU.add
                 )
+            else:
+                nc.scalar.activation(out=dst, in_=src, func=ACT.Identity, bias=bias[:, col : col + 1], scale=1.0)
+
+        def quantise_q(ph, j0, j1):
+            nc.vector.quantize_mx(
+                out=q_codes[ph][:, 128 * j0 : 128 * j1].bitcast(FP8X4),
+                scales=q_scales[ph][:, 128 * j0 : 128 * j1],
+                in_=q_grp[ph][:, 512 * j0 : 512 * j1],
+            )
 
         def second(g_ps, n):
             half, j = divmod(n, 4)
@@ -196,57 +161,115 @@ def tile_adaptivegraphconstruction_w_kernel(
                 stop=(n == 7),
             )
 
-        order = [(ph, i) for ph in range(4) for i in range(len(PIECES[ph]))]
+        def shared(bank, name):
+            t = psum.tile([P, 512], F32, tag="bank%d" % bank, name=name)
+            return (t[:, 0:TV], t[:, TV : 2 * TV], False)
+
+        def apart(bank0, bank1, name):
+            t0 = psum.tile([P, TV], F32, tag="bank%d" % bank0, name=name + "a")
+            t1 = psum.tile([P, TV], F32, tag="bank%d" % bank1, name=name + "b")
+            return (t0[:], t1[:], True)
+
+        nc.vector.memset(planes_raw[0][:].bitcast(I32), 0)
+        nc.vector.memset(stage[:], 0.0)
+        nc.vector.memset(warm_in[:], 0.0)
+        masks.make_identity(nc, ident[:])
+        for b in range(1, 4):
+            nc.gpsimd.memset(planes_raw[b][:].bitcast(I32), 0)
+        nc.scalar.dma_start(out=stage[0:8, :], in_=ba.rearrange("(i c) -> i c", c=256))
+        nc.scalar.dma_start(out=stage[8:16, :], in_=bb.rearrange("(i c) -> i c", c=256))
+        nc.scalar.dma_start(out=a_sb[:], in_=A[0])
+        nc.scalar.dma_start(out=alpha_bf[:], in_=alpha.partition_broadcast(P))
+        nc.scalar.activation(out=warm_out[:], in_=warm_in[:], func=ACT.Tanh)
+
         state = {"loaded": 0, "permuted": 0}
 
-        def advance(ph, i):
-            now = order.index((ph, i))
-            while state["loaded"] < min(now + 9, len(order)):
-                p2, i2 = order[state["loaded"]]
-                if (p2, i2) == (0, 4):
-                    load_scales(0, 1)
-                if p2 == 2 and i2 % 4 == 0:
-                    load_scales(1, i2 // 4)
-                load_w(p2, i2)
-                state["loaded"] += 1
-            lead = 4 if now < len(order) - 4 else 2
-            while state["permuted"] < min(now + lead, len(order)):
-                p2, i2 = order[state["permuted"]]
-                if p2 % 2 == 0 and i2 % 4 == 0:
-                    permute_scales(p2 + i2 // 4)
-                permute_w(p2, i2)
-                state["permuted"] += 1
+        def load_next():
+            ph, i = ORDER[state["loaded"]]
+            state["loaded"] += 1
+            if (ph, i) == (0, 0):
+                load_x(0)
+                load_scales(0, 0)
+            elif ph == 0:
+                load_x(i)
+            if (ph, i) == (0, 3):
+                load_scales(0, 1)
+            if (ph, i) == (1, 7):
+                load_scales(1, 0)
+            if (ph, i) == (2, 2):
+                load_scales(1, 1)
+            load_w(ph, i)
 
+        def permute_next():
+            ph, i = ORDER[state["permuted"]]
+            state["permuted"] += 1
+            if ph == 0:
+                regroup_x(i)
+            if ph % 2 == 0 and i % 4 == 0:
+                permute_scales(ph + i // 4)
+            if ph == 0:
+                quantise_x(i)
+            permute_w(ph, i)
+
+        def advance(ph, i, lead=3):
+            now = ORDER.index((ph, i))
+            while state["loaded"] < min(now + 9, len(ORDER)):
+                load_next()
+            while state["permuted"] < min(now + lead, len(ORDER)):
+                permute_next()
+
+        advance(0, 0, lead=1)
+
+        nc.vector.tensor_copy(out=stage_p[:].rearrange(joined, h=2, r=8), in_=stage[:].rearrange(split, h=2, r=8))
+        bt_ps = psum.tile([P, 256], BF16, tag="bank7", name="bt_ps")
+        for h in range(2):
+            nc.tensor.transpose(bt_ps[:, 128 * h : 128 * (h + 1)], stage_p[:, 128 * h : 128 * (h + 1)], ident[:])
+        for h in range(2):
+            nc.vector.tensor_copy(out=bias[:, 16 * h : 16 * (h + 1)], in_=bt_ps[:, 128 * h : 128 * h + 16])
+        nc.vector.tensor_copy(out=alpha_f[:], in_=alpha_bf[:])
+
+        prev = None
         for ph in range(3):
-            banks = [psum.tile([P, TV], F32, tag="bank%d" % i, name="acc%d_%d" % (ph, i)) for i in range(8)]
-            for g in range(GROUPS):
-                advance(ph, g)
-                passes(ph, g, banks)
+            acc = [shared(4 * (ph % 2) + j, "acc%d_%d" % (ph, j)) for j in range(4)]
+            for i in range(GROUPS):
+                advance(ph, i)
+                passes(ph, i, acc)
+                if i == 4 and ph > 0:
+                    quantise_q(ph - 1, 0, 4)
             for j in range(4):
-                evacuate(ph, banks, j)
-            quantise_q(ph, 0, 4)
+                for u in range(2):
+                    evacuate(ph, acc, j, u, ph == 2 and j == 0)
 
-        banks = [psum.tile([P, TV], F32, tag="bank%d" % i, name="acc3_%d" % i) for i in range(8)]
-        for piece in range(8):
-            advance(3, piece)
-            passes(3, piece, banks)
-        evacuate(3, banks, 0)
-        evacuate(3, banks, 1)
-        quantise_q(3, 0, 2)
-        advance(3, 8)
-        passes(3, 8, banks)
-        g_ps = psum.tile([P, V], F32, tag="bank0", name="g_ps")
+        acc = [shared(4, "acc3_0"), shared(5, "acc3_1"), apart(6, 7, "acc3_2"), apart(0, 1, "acc3_3")]
+        for i in range(6):
+            advance(3, i)
+            passes(3, i, acc)
+            if i == 4:
+                quantise_q(2, 0, 4)
+        g_ps = psum.tile([P, V], F32, tag="bank2", name="g_ps")
         for n in range(4):
             second(g_ps, n)
-        advance(3, 9)
-        passes(3, 9, banks)
-        evacuate(3, banks, 2, False)
-        advance(3, 10)
-        passes(3, 10, banks)
-        evacuate(3, banks, 3, True)
-        quantise_q(3, 2, 4)
-        for n in range(4, 8):
-            second(g_ps, n)
+        for i in (6, 7):
+            advance(3, i, 2)
+            passes(3, i, acc)
+        for u in range(2):
+            evacuate(3, acc, 0, u, False)
+            evacuate(3, acc, 1, u, True)
+        quantise_q(3, 0, 2)
+        for i in (8, 9):
+            advance(3, i, 2)
+            passes(3, i, acc)
+        second(g_ps, 4)
+        second(g_ps, 5)
+        evacuate(3, acc, 2, 0, True)
+        evacuate(3, acc, 2, 1, False)
+        passes(3, 10, acc)
+        evacuate(3, acc, 3, 0, True)
+        evacuate(3, acc, 3, 1, False)
+        quantise_q(3, 2, 3)
+        quantise_q(3, 3, 4)
+        second(g_ps, 6)
+        second(g_ps, 7)
 
         th = keep.tile([P, V], F32, name="th")
         z = keep.tile([P, V], F32, name="z")

@@ -21,10 +21,15 @@ TV = T * V
 GROUPS = C // 512
 FLOPS = 2 * 2 * IC * C * TV + 2 * V * V * IC * T
 
-WHOLE = [(g, 0, 4) for g in range(GROUPS)]
-PIECES = [WHOLE, WHOLE, WHOLE, WHOLE[:6] + [(6, 0, 2), (7, 0, 2), (6, 2, 2), (7, 2, 1), (7, 3, 1)]]
-ORDER = [(ph, i) for ph in range(4) for i in range(len(PIECES[ph]))]
-
+PIECES = (
+    [(0, 0, 0, 4), (0, 0, 4, 4)]
+    + [(0, g, 0, 8) for g in range(1, 6)]
+    + [(0, 6, 0, 4), (0, 7, 0, 4), (0, 6, 4, 4), (0, 7, 4, 4)]
+    + [(1, 0, 0, 4), (1, 1, 0, 4), (1, 0, 4, 4), (1, 1, 4, 4)]
+    + [(1, g, 0, 8) for g in range(2, 6)]
+    + [(1, 6, 0, 4), (1, 7, 0, 4), (1, 6, 4, 4), (1, 7, 4, 2), (1, 7, 6, 1), (1, 7, 7, 1)]
+)
+UNITS = [(i, j, min(4, n - (j - j0))) for i, (m, g, j0, n) in enumerate(PIECES) for j in range(j0, j0 + n, 4)]
 
 def tile_adaptivegraphconstruction_w_kernel(
     tc, x, Wa_words, Wa_scales, ba, Wb_words, Wb_scales, bb, A, alpha, out
@@ -34,7 +39,7 @@ def tile_adaptivegraphconstruction_w_kernel(
     scales = (Wa_scales, Wb_scales)
     with ExitStack() as ctx:
         keep = ctx.enter_context(tc.tile_pool(name="keep", bufs=1))
-        raw_pool = ctx.enter_context(tc.tile_pool(name="raw", bufs=10))
+        raw_pool = ctx.enter_context(tc.tile_pool(name="raw", bufs=7))
         w_pool = ctx.enter_context(tc.tile_pool(name="w", bufs=8))
         psum = ctx.enter_context(tc.psum_pool(name="psum", bufs=1))
         ctx.enter_context(tc.manual_schedule())
@@ -54,9 +59,9 @@ def tile_adaptivegraphconstruction_w_kernel(
         x_grp = [keep.tile([P, 4 * TV], BF16, name="x_grp%d" % g, align_bytes=64) for g in range(GROUPS)]
         x_codes = [keep.tile([P, TV], I32, name="x_codes%d" % g, align_bytes=64) for g in range(GROUPS)]
         x_scales = [keep.tile([P, TV], U8, name="x_scales%d" % g, align_bytes=64) for g in range(GROUPS)]
-        q_grp = [keep.tile([P, 2048], BF16, name="q_grp%d" % ph, align_bytes=64) for ph in range(4)]
-        q_codes = [keep.tile([P, 512], I32, name="q_codes%d" % ph, align_bytes=64) for ph in range(4)]
-        q_scales = [keep.tile([P, 512], U8, name="q_scales%d" % ph, align_bytes=64) for ph in range(4)]
+        q_grp = [keep.tile([P, 4096], BF16, name="q_grp%d" % m, align_bytes=64) for m in range(2)]
+        q_codes = [keep.tile([P, 1024], I32, name="q_codes%d" % m, align_bytes=64) for m in range(2)]
+        q_scales = [keep.tile([P, 1024], U8, name="q_scales%d" % m, align_bytes=64) for m in range(2)]
         w_raw = {}
         w = {}
 
@@ -65,13 +70,11 @@ def tile_adaptivegraphconstruction_w_kernel(
         def load_x(g):
             nc.sync.dma_start(out=x_raw[g][:], in_=xv[g])
 
-        def load_w(ph, i):
-            wsel, half = divmod(ph, 2)
-            g, j0, n = PIECES[ph][i]
-            first = 4096 * half + 1024 * j0
-            src = words[wsel][g].rearrange("p n t -> p (n t)")[:, first : first + 1024 * n]
-            raw = raw_pool.tile([P, 1024], I32, name="raw", align_bytes=64)
-            w_raw[ph, i] = raw
+        def load_w(i):
+            m, g, j0, n = PIECES[i]
+            src = words[m][g].rearrange("p n t -> p (n t)")[:, 1024 * j0 : 1024 * (j0 + n)]
+            raw = raw_pool.tile([P, 2048], I32, name="raw", align_bytes=64)
+            w_raw[i] = raw
             nc.sync.dma_start(out=raw[:, 0 : 256 * n], in_=src.bitcast(I32))
 
         def load_scales(wsel, b):
@@ -90,13 +93,14 @@ def tile_adaptivegraphconstruction_w_kernel(
                 in_=planes_raw[b][:].bitcast(I32).rearrange(split, h=2, r=2),
             )
 
-        def permute_w(ph, i):
-            n = PIECES[ph][i][2]
+        def permute_w(unit):
+            i, j, n = UNITS[unit]
+            at = 256 * (j - PIECES[i][2])
             tile = w_pool.tile([P, 1024], I32, name="w", align_bytes=64)
-            w[ph, i] = tile
+            w[unit] = tile
             nc.vector.tensor_copy(
                 out=tile[:, 0 : 256 * n].rearrange(joined, h=2, r=8),
-                in_=w_raw[ph, i][:, 0 : 256 * n].rearrange(split, h=2, r=8),
+                in_=w_raw[i][:, at : at + 256 * n].rearrange(split, h=2, r=8),
             )
 
         def regroup_x(g):
@@ -110,65 +114,59 @@ def tile_adaptivegraphconstruction_w_kernel(
         def quantise_x(g):
             nc.vector.quantize_mx(out=x_codes[g][:].bitcast(FP8X4), scales=x_scales[g][:], in_=x_grp[g][:])
 
-        def passes(ph, i, acc):
-            wsel, half = divmod(ph, 2)
-            g, j0, n = PIECES[ph][i]
-            blk = planes[2 * wsel + g // 4]
+        def passes(unit, acc):
+            i, j0, n = UNITS[unit]
+            m, g = PIECES[i][0:2]
             k = 4 * (g % 4)
             for j in range(j0, j0 + n):
                 for u in range(2):
-                    col = 1024 * u + 512 * half + 128 * j
+                    col = 1024 * u + 128 * j
                     at = 128 * n * u + 128 * (j - j0)
                     nc.tensor.matmul_mx(
-                        out=acc[j][u],
-                        lhsT=w[ph, i][:, at : at + 128].bitcast(FP8X4),
-                        lhsT_scale=blk[k:P, col : col + 128],
+                        out=acc[j][:, TV * u : TV * (u + 1)],
+                        lhsT=w[unit][:, at : at + 128].bitcast(FP8X4),
+                        lhsT_scale=planes[2 * m + g // 4][k:P, col : col + 128],
                         rhs=x_codes[g][:].bitcast(FP8X4),
                         rhs_scale=x_scales[g][:],
-                        start=(g == 0 and (u == 0 or acc[j][2])),
-                        stop=(g == GROUPS - 1 and (u == 1 or acc[j][2])),
+                        start=(g == 0 and u == 0),
+                        stop=(g == GROUPS - 1 and u == 1),
                     )
 
-        def evacuate(ph, acc, j, u, on_vector):
-            wsel, half = divmod(ph, 2)
-            src = acc[j][u].rearrange("p (t v) -> p v t", t=T)
-            dst = q_grp[ph][:].rearrange("p (j v c) -> p j v c", j=4, c=4)[:, j, :, 2 * u : 2 * u + 2]
-            col = 16 * u + 8 * wsel + 4 * half + j
+        def evacuate(m, acc, j, on_vector):
+            dst = q_grp[m][:, 512 * j : 512 * (j + 1)].rearrange("p (v u t) -> p v u t", u=2, t=T)
+            src = acc[j][:].rearrange("p (u t v) -> p v u t", u=2, t=T)
+            row = 16 * m + 2 * j
             if on_vector:
-                nc.vector.tensor_scalar(
-                    out=dst, in0=src, scalar1=bias[:, col : col + 1], scalar2=None, op0=ALU.add
-                )
+                both = bias[:, row : row + 2].unsqueeze(1).unsqueeze(3).to_broadcast([P, V, 2, T])
+                nc.vector.tensor_tensor(out=dst, in0=src, in1=both, op=ALU.add)
             else:
-                nc.scalar.activation(out=dst, in_=src, func=ACT.Identity, bias=bias[:, col : col + 1], scale=1.0)
+                for u in range(2):
+                    nc.scalar.activation(
+                        out=dst[:, :, u, :],
+                        in_=src[:, :, u, :],
+                        func=ACT.Identity,
+                        bias=bias[:, row + u : row + u + 1],
+                        scale=1.0,
+                    )
 
-        def quantise_q(ph, j0, j1):
+        def quantise_q(m, j0, j1):
             nc.vector.quantize_mx(
-                out=q_codes[ph][:, 128 * j0 : 128 * j1].bitcast(FP8X4),
-                scales=q_scales[ph][:, 128 * j0 : 128 * j1],
-                in_=q_grp[ph][:, 512 * j0 : 512 * j1],
+                out=q_codes[m][:, 128 * j0 : 128 * j1].bitcast(FP8X4),
+                scales=q_scales[m][:, 128 * j0 : 128 * j1],
+                in_=q_grp[m][:, 512 * j0 : 512 * j1],
             )
 
-        def second(g_ps, n):
-            half, j = divmod(n, 4)
+        def second(g_ps, j):
             cols = slice(128 * j, 128 * (j + 1))
             nc.tensor.matmul_mx(
                 out=g_ps[:],
-                lhsT=q_codes[half][:, cols].bitcast(FP8X4),
-                lhsT_scale=q_scales[half][:, cols],
-                rhs=q_codes[2 + half][:, cols].bitcast(FP8X4),
-                rhs_scale=q_scales[2 + half][:, cols],
-                start=(n == 0),
-                stop=(n == 7),
+                lhsT=q_codes[0][:, cols].bitcast(FP8X4),
+                lhsT_scale=q_scales[0][:, cols],
+                rhs=q_codes[1][:, cols].bitcast(FP8X4),
+                rhs_scale=q_scales[1][:, cols],
+                start=(j == 0),
+                stop=(j == 7),
             )
-
-        def shared(bank, name):
-            t = psum.tile([P, 512], F32, tag="bank%d" % bank, name=name)
-            return (t[:, 0:TV], t[:, TV : 2 * TV], False)
-
-        def apart(bank0, bank1, name):
-            t0 = psum.tile([P, TV], F32, tag="bank%d" % bank0, name=name + "a")
-            t1 = psum.tile([P, TV], F32, tag="bank%d" % bank1, name=name + "b")
-            return (t0[:], t1[:], True)
 
         nc.vector.memset(planes_raw[0][:].bitcast(I32), 0)
         nc.vector.memset(stage[:], 0.0)
@@ -182,92 +180,96 @@ def tile_adaptivegraphconstruction_w_kernel(
         nc.scalar.dma_start(out=alpha_bf[:], in_=alpha.partition_broadcast(P))
         nc.scalar.activation(out=warm_out[:], in_=warm_in[:], func=ACT.Tanh)
 
+        load_x(0)
+        load_scales(0, 0)
+        load_x(1)
         state = {"loaded": 0, "permuted": 0}
 
         def load_next():
-            ph, i = ORDER[state["loaded"]]
+            i = state["loaded"]
             state["loaded"] += 1
-            if (ph, i) == (0, 0):
-                load_x(0)
-                load_scales(0, 0)
-            elif ph == 0:
-                load_x(i)
-            if (ph, i) == (0, 3):
+            m, g, j0, n = PIECES[i]
+            if m == 0 and j0 == 0 and 1 <= g < 7:
+                load_x(g + 1)
+            if (m, g, j0) == (0, 2, 0):
                 load_scales(0, 1)
-            if (ph, i) == (1, 7):
+            if (m, g, j0) == (0, 6, 4):
                 load_scales(1, 0)
-            if (ph, i) == (2, 2):
+            if (m, g, j0) == (1, 2, 0):
                 load_scales(1, 1)
-            load_w(ph, i)
+            load_w(i)
 
         def permute_next():
-            ph, i = ORDER[state["permuted"]]
+            unit = state["permuted"]
             state["permuted"] += 1
-            if ph == 0:
-                regroup_x(i)
-            if ph % 2 == 0 and i % 4 == 0:
-                permute_scales(ph + i // 4)
-            if ph == 0:
-                quantise_x(i)
-            permute_w(ph, i)
+            i, j, n = UNITS[unit]
+            m, g = PIECES[i][0:2]
+            if m == 0 and j == 0:
+                regroup_x(g)
+            if g % 4 == 0 and j == 0:
+                permute_scales(2 * m + g // 4)
+            if m == 0 and j == 0:
+                quantise_x(g)
+            permute_w(unit)
 
-        def advance(ph, i, lead=3):
-            now = ORDER.index((ph, i))
-            while state["loaded"] < min(now + 9, len(ORDER)):
+        def advance(unit, lead):
+            while state["loaded"] < min(UNITS[unit][0] + 6, len(PIECES)):
                 load_next()
-            while state["permuted"] < min(now + lead, len(ORDER)):
+            while state["permuted"] < min(unit + 1 + lead, len(UNITS)):
                 permute_next()
 
-        advance(0, 0, lead=1)
+        def run(first, last, acc, lead):
+            for unit in range(first, last):
+                advance(unit, lead)
+                passes(unit, acc)
+
+        def unit_after(m, g, j):
+            return 1 + [(PIECES[i][0], PIECES[i][1]) == (m, g) and j0 <= j < j0 + n for i, j0, n in UNITS].index(True)
+
+        advance(0, 0)
 
         nc.vector.tensor_copy(out=stage_p[:].rearrange(joined, h=2, r=8), in_=stage[:].rearrange(split, h=2, r=8))
-        bt_ps = psum.tile([P, 256], BF16, tag="bank7", name="bt_ps")
+        bt_ps = psum.tile([P, 2, P], BF16, tag="bank7", name="bt_ps")
         for h in range(2):
-            nc.tensor.transpose(bt_ps[:, 128 * h : 128 * (h + 1)], stage_p[:, 128 * h : 128 * (h + 1)], ident[:])
-        for h in range(2):
-            nc.vector.tensor_copy(out=bias[:, 16 * h : 16 * (h + 1)], in_=bt_ps[:, 128 * h : 128 * h + 16])
+            nc.tensor.transpose(bt_ps[:, h, :], stage_p[:, 128 * h : 128 * (h + 1)], ident[:])
+        nc.vector.tensor_copy(
+            out=bias[:].rearrange("p (i h) -> p i h", h=2), in_=bt_ps[:, :, 0:16].rearrange("p h i -> p i h")
+        )
         nc.vector.tensor_copy(out=alpha_f[:], in_=alpha_bf[:])
 
-        prev = None
-        for ph in range(3):
-            acc = [shared(4 * (ph % 2) + j, "acc%d_%d" % (ph, j)) for j in range(4)]
-            for i in range(GROUPS):
-                advance(ph, i)
-                passes(ph, i, acc)
-                if i == 4 and ph > 0:
-                    quantise_q(ph - 1, 0, 4)
-            for j in range(4):
-                for u in range(2):
-                    evacuate(ph, acc, j, u, ph == 2 and j == 0)
+        acc = [psum.tile([P, 512], F32, tag="bank%d" % j, name="acc_a%d" % j) for j in range(8)]
+        done = unit_after(0, 7, 0)
+        run(0, done, acc, 2)
+        for j in range(4):
+            evacuate(0, acc, j, j % 2 == 1)
+        run(done, unit_after(0, 7, 4), acc, 2)
+        for j in range(4, 8):
+            evacuate(0, acc, j, j % 2 == 1)
 
-        acc = [shared(4, "acc3_0"), shared(5, "acc3_1"), apart(6, 7, "acc3_2"), apart(0, 1, "acc3_3")]
-        for i in range(6):
-            advance(3, i)
-            passes(3, i, acc)
-            if i == 4:
-                quantise_q(2, 0, 4)
-        g_ps = psum.tile([P, V], F32, tag="bank2", name="g_ps")
-        for n in range(4):
-            second(g_ps, n)
-        for i in (6, 7):
-            advance(3, i, 2)
-            passes(3, i, acc)
-        for u in range(2):
-            evacuate(3, acc, 0, u, False)
-            evacuate(3, acc, 1, u, True)
-        quantise_q(3, 0, 2)
-        for i in (8, 9):
-            advance(3, i, 2)
-            passes(3, i, acc)
+        done = unit_after(0, 7, 4)
+        acc = [psum.tile([P, 512], F32, tag="bank%d" % j, name="acc_b%d" % j) for j in range(8)]
+        run(done, done + 4, acc, 2)
+        quantise_q(0, 0, 4)
+        quantise_q(0, 4, 8)
+        run(done + 4, unit_after(1, 7, 0), acc, 1)
+        for j in range(4):
+            evacuate(1, acc, j, j % 2 == 1)
+        run(unit_after(1, 7, 0), unit_after(1, 7, 4), acc, 1)
+        g_ps = psum.tile([P, V], F32, tag="bank0", name="g_ps")
+        quantise_q(1, 0, 4)
+        evacuate(1, acc, 4, False)
+        evacuate(1, acc, 5, True)
+        for j in range(4):
+            second(g_ps, j)
+        run(unit_after(1, 7, 4), unit_after(1, 7, 6), acc, 1)
+        evacuate(1, acc, 6, False)
+        quantise_q(1, 4, 6)
         second(g_ps, 4)
         second(g_ps, 5)
-        evacuate(3, acc, 2, 0, True)
-        evacuate(3, acc, 2, 1, False)
-        passes(3, 10, acc)
-        evacuate(3, acc, 3, 0, True)
-        evacuate(3, acc, 3, 1, False)
-        quantise_q(3, 2, 3)
-        quantise_q(3, 3, 4)
+        run(unit_after(1, 7, 6), len(UNITS), acc, 1)
+        evacuate(1, acc, 7, True)
+        quantise_q(1, 6, 7)
+        quantise_q(1, 7, 8)
         second(g_ps, 6)
         second(g_ps, 7)
 

@@ -22,14 +22,13 @@ GROUPS = C // 512
 FLOPS = 2 * 2 * IC * C * TV + 2 * V * V * IC * T
 
 PIECES = (
-    [(0, 0, 0, 4), (0, 0, 4, 4)]
-    + [(0, g, 0, 8) for g in range(1, 6)]
-    + [(0, 6, 0, 4), (0, 7, 0, 4), (0, 6, 4, 4), (0, 7, 4, 4)]
-    + [(1, 0, 0, 4), (1, 1, 0, 4), (1, 0, 4, 4), (1, 1, 4, 4)]
-    + [(1, g, 0, 8) for g in range(2, 6)]
-    + [(1, 6, 0, 4), (1, 7, 0, 4), (1, 6, 4, 4), (1, 7, 4, 2), (1, 7, 6, 1), (1, 7, 7, 1)]
+    [(0, 0, 0, 2), (0, 0, 2, 2), (0, 0, 4, 4)]
+    + [(0, g, j, 4) for g in range(1, 4) for j in (0, 4)]
+    + [(0, g, j, 4) for j in (0, 4) for g in range(4, 8)]
+    + [(1, g, j, 4) for j in (0, 4) for g in range(4)]
+    + [(1, g, 0, 4) for g in range(4, 8)]
+    + [(1, 4, 4, 4), (1, 5, 4, 4), (1, 6, 4, 2), (1, 7, 4, 2), (1, 6, 6, 2), (1, 7, 6, 1), (1, 7, 7, 1)]
 )
-UNITS = [(i, j, min(4, n - (j - j0))) for i, (m, g, j0, n) in enumerate(PIECES) for j in range(j0, j0 + n, 4)]
 
 def tile_adaptivegraphconstruction_w_kernel(
     tc, x, Wa_words, Wa_scales, ba, Wb_words, Wb_scales, bb, A, alpha, out
@@ -39,7 +38,7 @@ def tile_adaptivegraphconstruction_w_kernel(
     scales = (Wa_scales, Wb_scales)
     with ExitStack() as ctx:
         keep = ctx.enter_context(tc.tile_pool(name="keep", bufs=1))
-        raw_pool = ctx.enter_context(tc.tile_pool(name="raw", bufs=7))
+        raw_pool = ctx.enter_context(tc.tile_pool(name="raw", bufs=14))
         w_pool = ctx.enter_context(tc.tile_pool(name="w", bufs=8))
         psum = ctx.enter_context(tc.psum_pool(name="psum", bufs=1))
         ctx.enter_context(tc.manual_schedule())
@@ -73,7 +72,7 @@ def tile_adaptivegraphconstruction_w_kernel(
         def load_w(i):
             m, g, j0, n = PIECES[i]
             src = words[m][g].rearrange("p n t -> p (n t)")[:, 1024 * j0 : 1024 * (j0 + n)]
-            raw = raw_pool.tile([P, 2048], I32, name="raw", align_bytes=64)
+            raw = raw_pool.tile([P, 1024], I32, name="raw", align_bytes=64)
             w_raw[i] = raw
             nc.sync.dma_start(out=raw[:, 0 : 256 * n], in_=src.bitcast(I32))
 
@@ -93,14 +92,13 @@ def tile_adaptivegraphconstruction_w_kernel(
                 in_=planes_raw[b][:].bitcast(I32).rearrange(split, h=2, r=2),
             )
 
-        def permute_w(unit):
-            i, j, n = UNITS[unit]
-            at = 256 * (j - PIECES[i][2])
+        def permute_w(i):
+            n = PIECES[i][3]
             tile = w_pool.tile([P, 1024], I32, name="w", align_bytes=64)
-            w[unit] = tile
+            w[i] = tile
             nc.vector.tensor_copy(
                 out=tile[:, 0 : 256 * n].rearrange(joined, h=2, r=8),
-                in_=w_raw[i][:, at : at + 256 * n].rearrange(split, h=2, r=8),
+                in_=w_raw[i][:, 0 : 256 * n].rearrange(split, h=2, r=8),
             )
 
         def regroup_x(g):
@@ -114,9 +112,8 @@ def tile_adaptivegraphconstruction_w_kernel(
         def quantise_x(g):
             nc.vector.quantize_mx(out=x_codes[g][:].bitcast(FP8X4), scales=x_scales[g][:], in_=x_grp[g][:])
 
-        def passes(unit, acc):
-            i, j0, n = UNITS[unit]
-            m, g = PIECES[i][0:2]
+        def passes(i, acc):
+            m, g, j0, n = PIECES[i]
             k = 4 * (g % 4)
             for j in range(j0, j0 + n):
                 for u in range(2):
@@ -124,7 +121,7 @@ def tile_adaptivegraphconstruction_w_kernel(
                     at = 128 * n * u + 128 * (j - j0)
                     nc.tensor.matmul_mx(
                         out=acc[j][:, TV * u : TV * (u + 1)],
-                        lhsT=w[unit][:, at : at + 128].bitcast(FP8X4),
+                        lhsT=w[i][:, at : at + 128].bitcast(FP8X4),
                         lhsT_scale=planes[2 * m + g // 4][k:P, col : col + 128],
                         rhs=x_codes[g][:].bitcast(FP8X4),
                         rhs_scale=x_scales[g][:],
@@ -176,57 +173,50 @@ def tile_adaptivegraphconstruction_w_kernel(
             nc.gpsimd.memset(planes_raw[b][:].bitcast(I32), 0)
         nc.scalar.dma_start(out=stage[0:8, :], in_=ba.rearrange("(i c) -> i c", c=256))
         nc.scalar.dma_start(out=stage[8:16, :], in_=bb.rearrange("(i c) -> i c", c=256))
-        nc.scalar.dma_start(out=a_sb[:], in_=A[0])
-        nc.scalar.dma_start(out=alpha_bf[:], in_=alpha.partition_broadcast(P))
         nc.scalar.activation(out=warm_out[:], in_=warm_in[:], func=ACT.Tanh)
 
         load_x(0)
         load_scales(0, 0)
-        load_x(1)
         state = {"loaded": 0, "permuted": 0}
 
         def load_next():
             i = state["loaded"]
             state["loaded"] += 1
             m, g, j0, n = PIECES[i]
-            if m == 0 and j0 == 0 and 1 <= g < 7:
+            if m == 0 and j0 == (2 if g == 0 else 4 if g < 4 else 0) and g < 7:
                 load_x(g + 1)
             if (m, g, j0) == (0, 2, 0):
                 load_scales(0, 1)
-            if (m, g, j0) == (0, 6, 4):
+            if (m, g, j0) == (0, 5, 4):
                 load_scales(1, 0)
-            if (m, g, j0) == (1, 2, 0):
+            if (m, g, j0) == (1, 1, 4):
                 load_scales(1, 1)
             load_w(i)
 
         def permute_next():
-            unit = state["permuted"]
+            i = state["permuted"]
             state["permuted"] += 1
-            i, j, n = UNITS[unit]
-            m, g = PIECES[i][0:2]
-            if m == 0 and j == 0:
+            m, g, j0, n = PIECES[i]
+            if m == 0 and j0 == 0:
                 regroup_x(g)
-            if g % 4 == 0 and j == 0:
+            if g % 4 == 0 and j0 == 0:
                 permute_scales(2 * m + g // 4)
-            if m == 0 and j == 0:
+            if m == 0 and j0 == 0:
                 quantise_x(g)
-            permute_w(unit)
+            permute_w(i)
 
-        def advance(unit, lead):
-            while state["loaded"] < min(UNITS[unit][0] + 6, len(PIECES)):
-                load_next()
-            while state["permuted"] < min(unit + 1 + lead, len(UNITS)):
-                permute_next()
+        def run(first, last, acc, lead=2, between=()):
+            for i in range(first, last):
+                while state["loaded"] < min(i + 12, len(PIECES)):
+                    load_next()
+                while state["permuted"] < min(i + 1 + lead, len(PIECES)):
+                    permute_next()
+                passes(i, acc)
+                if i - first < len(between):
+                    between[i - first]()
 
-        def run(first, last, acc, lead):
-            for unit in range(first, last):
-                advance(unit, lead)
-                passes(unit, acc)
-
-        def unit_after(m, g, j):
-            return 1 + [(PIECES[i][0], PIECES[i][1]) == (m, g) and j0 <= j < j0 + n for i, j0, n in UNITS].index(True)
-
-        advance(0, 0)
+        acc = [psum.tile([P, 512], F32, tag="bank%d" % j, name="acc_a%d" % j) for j in range(4)]
+        run(0, 2, acc, 0)
 
         nc.vector.tensor_copy(out=stage_p[:].rearrange(joined, h=2, r=8), in_=stage[:].rearrange(split, h=2, r=8))
         bt_ps = psum.tile([P, 2, P], BF16, tag="bank7", name="bt_ps")
@@ -235,43 +225,45 @@ def tile_adaptivegraphconstruction_w_kernel(
         nc.vector.tensor_copy(
             out=bias[:].rearrange("p (i h) -> p i h", h=2), in_=bt_ps[:, :, 0:16].rearrange("p h i -> p i h")
         )
+
+        acc_a = acc + [psum.tile([P, 512], F32, tag="bank%d" % j, name="acc_a%d" % j) for j in range(4, 8)]
+        low_a = PIECES.index((0, 7, 0, 4)) + 1
+        low_b = PIECES.index((1, 7, 0, 4)) + 1
+        first_b = PIECES.index((1, 0, 0, 4))
+
+        def empty(m, acc, j0):
+            evacuate(m, acc, j0, False)
+            evacuate(m, acc, j0 + 2, False)
+            return [
+                lambda: evacuate(m, acc, j0 + 1, True),
+                lambda: evacuate(m, acc, j0 + 3, True),
+                lambda: quantise_q(m, j0, j0 + 4),
+            ]
+
+        run(2, low_a, acc_a)
+        nc.scalar.dma_start(out=a_sb[:], in_=A[0])
+        nc.scalar.dma_start(out=alpha_bf[:], in_=alpha.partition_broadcast(P))
+        run(low_a, first_b, acc_a, between=empty(0, acc_a, 0))
+
         nc.vector.tensor_copy(out=alpha_f[:], in_=alpha_bf[:])
-
-        acc = [psum.tile([P, 512], F32, tag="bank%d" % j, name="acc_a%d" % j) for j in range(8)]
-        done = unit_after(0, 7, 0)
-        run(0, done, acc, 2)
-        for j in range(4):
-            evacuate(0, acc, j, j % 2 == 1)
-        run(done, unit_after(0, 7, 4), acc, 2)
-        for j in range(4, 8):
-            evacuate(0, acc, j, j % 2 == 1)
-
-        done = unit_after(0, 7, 4)
-        acc = [psum.tile([P, 512], F32, tag="bank%d" % j, name="acc_b%d" % j) for j in range(8)]
-        run(done, done + 4, acc, 2)
-        quantise_q(0, 0, 4)
-        quantise_q(0, 4, 8)
-        run(done + 4, unit_after(1, 7, 0), acc, 1)
-        for j in range(4):
-            evacuate(1, acc, j, j % 2 == 1)
-        run(unit_after(1, 7, 0), unit_after(1, 7, 4), acc, 1)
-        g_ps = psum.tile([P, V], F32, tag="bank0", name="g_ps")
-        quantise_q(1, 0, 4)
-        evacuate(1, acc, 4, False)
-        evacuate(1, acc, 5, True)
-        for j in range(4):
-            second(g_ps, j)
-        run(unit_after(1, 7, 4), unit_after(1, 7, 6), acc, 1)
-        evacuate(1, acc, 6, False)
+        todo = empty(0, acc_a, 4)
+        acc_b = [psum.tile([P, 512], F32, tag="bank%d" % j, name="acc_b%d" % j) for j in range(4)]
+        run(first_b, first_b + 4, acc_b, between=todo)
+        acc_b += [psum.tile([P, 512], F32, tag="bank%d" % j, name="acc_b%d" % j) for j in range(4, 8)]
+        run(first_b + 4, low_b, acc_b)
+        run(low_b, low_b + 4, acc_b, between=empty(1, acc_b, 0))
+        evacuate(1, acc_b, 5, False)
+        run(low_b + 4, low_b + 6, acc_b)
+        evacuate(1, acc_b, 4, True)
+        evacuate(1, acc_b, 6, True)
+        run(low_b + 6, len(PIECES), acc_b)
         quantise_q(1, 4, 6)
-        second(g_ps, 4)
-        second(g_ps, 5)
-        run(unit_after(1, 7, 6), len(UNITS), acc, 1)
-        evacuate(1, acc, 7, True)
+        evacuate(1, acc_b, 7, True)
         quantise_q(1, 6, 7)
         quantise_q(1, 7, 8)
-        second(g_ps, 6)
-        second(g_ps, 7)
+        g_ps = psum.tile([P, V], F32, tag="bank0", name="g_ps")
+        for j in range(8):
+            second(g_ps, j)
 
         th = keep.tile([P, V], F32, name="th")
         z = keep.tile([P, V], F32, name="z")

@@ -27,7 +27,7 @@ PIECES = (
     + [(0, g, j, 4) for j in (0, 4) for g in range(4, 8)]
     + [(1, g, j, 4) for j in (0, 4) for g in range(4)]
     + [(1, g, 0, 4) for g in range(4, 8)]
-    + [(1, 4, 4, 4), (1, 5, 4, 4), (1, 6, 4, 2), (1, 7, 4, 2), (1, 6, 6, 2), (1, 7, 6, 1), (1, 7, 7, 1)]
+    + [(1, 4, 4, 4), (1, 5, 4, 2), (1, 6, 4, 2), (1, 7, 4, 2), (1, 5, 6, 2), (1, 6, 6, 2), (1, 7, 6, 1), (1, 7, 7, 1)]
 )
 
 def tile_adaptivegraphconstruction_w_kernel(
@@ -171,27 +171,30 @@ def tile_adaptivegraphconstruction_w_kernel(
         masks.make_identity(nc, ident[:])
         for b in range(1, 4):
             nc.gpsimd.memset(planes_raw[b][:].bitcast(I32), 0)
-        nc.scalar.dma_start(out=stage[0:8, :], in_=ba.rearrange("(i c) -> i c", c=256))
-        nc.scalar.dma_start(out=stage[8:16, :], in_=bb.rearrange("(i c) -> i c", c=256))
         nc.scalar.activation(out=warm_out[:], in_=warm_in[:], func=ACT.Tanh)
 
-        load_x(0)
-        load_scales(0, 0)
         state = {"loaded": 0, "permuted": 0}
 
         def load_next():
             i = state["loaded"]
             state["loaded"] += 1
             m, g, j0, n = PIECES[i]
+            if i == 0:
+                load_x(0)
+                load_w(0)
+                load_scales(0, 0)
+                return
             if m == 0 and j0 == (2 if g == 0 else 4 if g < 4 else 0) and g < 7:
                 load_x(g + 1)
-            if (m, g, j0) == (0, 2, 0):
-                load_scales(0, 1)
-            if (m, g, j0) == (0, 5, 4):
-                load_scales(1, 0)
-            if (m, g, j0) == (1, 1, 4):
-                load_scales(1, 1)
+            if g % 4 == 0 and j0 == 0:
+                load_scales(m, g // 4)
+            if (m, g, j0) == (1, 0, 4):
+                nc.sync.dma_start(out=a_sb[:], in_=A[0])
+                nc.sync.dma_start(out=alpha_bf[:], in_=alpha.partition_broadcast(P))
             load_w(i)
+            if i == 1:
+                nc.sync.dma_start(out=stage[0:8, :], in_=ba.rearrange("(i c) -> i c", c=256))
+                nc.sync.dma_start(out=stage[8:16, :], in_=bb.rearrange("(i c) -> i c", c=256))
 
         def permute_next():
             i = state["permuted"]
@@ -215,18 +218,24 @@ def tile_adaptivegraphconstruction_w_kernel(
                 if i - first < len(between):
                     between[i - first]()
 
-        acc = [psum.tile([P, 512], F32, tag="bank%d" % j, name="acc_a%d" % j) for j in range(4)]
-        run(0, 2, acc, 0)
-
+        while state["loaded"] < 8:
+            load_next()
+        regroup_x(0)
+        permute_w(0)
+        quantise_x(0)
+        permute_scales(0)
+        state["permuted"] = 1
+        acc_a = [psum.tile([P, 512], F32, tag="bank%d" % j, name="acc_a%d" % j) for j in range(4)]
+        run(0, 2, acc_a, 0)
         nc.vector.tensor_copy(out=stage_p[:].rearrange(joined, h=2, r=8), in_=stage[:].rearrange(split, h=2, r=8))
+        permute_next()
         bt_ps = psum.tile([P, 2, P], BF16, tag="bank7", name="bt_ps")
         for h in range(2):
             nc.tensor.transpose(bt_ps[:, h, :], stage_p[:, 128 * h : 128 * (h + 1)], ident[:])
         nc.vector.tensor_copy(
             out=bias[:].rearrange("p (i h) -> p i h", h=2), in_=bt_ps[:, :, 0:16].rearrange("p h i -> p i h")
         )
-
-        acc_a = acc + [psum.tile([P, 512], F32, tag="bank%d" % j, name="acc_a%d" % j) for j in range(4, 8)]
+        acc_a += [psum.tile([P, 512], F32, tag="bank%d" % j, name="acc_a%d" % j) for j in range(4, 8)]
         low_a = PIECES.index((0, 7, 0, 4)) + 1
         low_b = PIECES.index((1, 7, 0, 4)) + 1
         first_b = PIECES.index((1, 0, 0, 4))
@@ -241,23 +250,22 @@ def tile_adaptivegraphconstruction_w_kernel(
             ]
 
         run(2, low_a, acc_a)
-        nc.scalar.dma_start(out=a_sb[:], in_=A[0])
-        nc.scalar.dma_start(out=alpha_bf[:], in_=alpha.partition_broadcast(P))
         run(low_a, first_b, acc_a, between=empty(0, acc_a, 0))
 
-        nc.vector.tensor_copy(out=alpha_f[:], in_=alpha_bf[:])
         todo = empty(0, acc_a, 4)
         acc_b = [psum.tile([P, 512], F32, tag="bank%d" % j, name="acc_b%d" % j) for j in range(4)]
         run(first_b, first_b + 4, acc_b, between=todo)
         acc_b += [psum.tile([P, 512], F32, tag="bank%d" % j, name="acc_b%d" % j) for j in range(4, 8)]
         run(first_b + 4, low_b, acc_b)
-        run(low_b, low_b + 4, acc_b, between=empty(1, acc_b, 0))
+        nc.vector.tensor_copy(out=alpha_f[:], in_=alpha_bf[:])
+        close = PIECES.index((1, 7, 4, 2)) + 1
+        run(low_b, close, acc_b, between=empty(1, acc_b, 0))
         evacuate(1, acc_b, 5, False)
-        run(low_b + 4, low_b + 6, acc_b)
         evacuate(1, acc_b, 4, True)
-        evacuate(1, acc_b, 6, True)
-        run(low_b + 6, len(PIECES), acc_b)
+        run(close, len(PIECES) - 1, acc_b)
         quantise_q(1, 4, 6)
+        evacuate(1, acc_b, 6, True)
+        run(len(PIECES) - 1, len(PIECES), acc_b)
         evacuate(1, acc_b, 7, True)
         quantise_q(1, 6, 7)
         quantise_q(1, 7, 8)

@@ -48,7 +48,6 @@ def tile_adaptivegraphconstruction_w_kernel(
         ident = keep.tile([P, P], BF16, name="ident")
         bias = keep.tile([P, 32], F32, name="bias")
         a_sb = keep.tile([P, V], BF16, name="a_sb")
-        alpha_bf = keep.tile([P, 1], BF16, name="alpha_bf")
         alpha_f = keep.tile([P, 1], F32, name="alpha_f")
         warm_in = keep.tile([P, 1], F32, name="warm_in")
         warm_out = keep.tile([P, 1], F32, name="warm_out")
@@ -186,15 +185,19 @@ def tile_adaptivegraphconstruction_w_kernel(
                 return
             if m == 0 and j0 == (2 if g == 0 else 4 if g < 4 else 0) and g < 7:
                 load_x(g + 1)
-            if g % 4 == 0 and j0 == 0:
-                load_scales(m, g // 4)
-            if (m, g, j0) == (1, 0, 4):
-                nc.sync.dma_start(out=a_sb[:], in_=A[0])
-                nc.sync.dma_start(out=alpha_bf[:], in_=alpha.partition_broadcast(P))
+            if (m, g, j0) == (0, 2, 0):
+                load_scales(0, 1)
+            if (m, g, j0) == (0, 5, 4):
+                load_scales(1, 0)
+            if (m, g, j0) == (1, 1, 4):
+                load_scales(1, 1)
             load_w(i)
+            if i == len(PIECES) - 1:
+                nc.sync.dma_start(out=a_sb[:], in_=A[0])
             if i == 1:
                 nc.sync.dma_start(out=stage[0:8, :], in_=ba.rearrange("(i c) -> i c", c=256))
                 nc.sync.dma_start(out=stage[8:16, :], in_=bb.rearrange("(i c) -> i c", c=256))
+                nc.sync.dma_start(out=stage[16:17, 0:1], in_=alpha.unsqueeze(0))
 
         def permute_next():
             i = state["permuted"]
@@ -229,12 +232,20 @@ def tile_adaptivegraphconstruction_w_kernel(
         run(0, 2, acc_a, 0)
         nc.vector.tensor_copy(out=stage_p[:].rearrange(joined, h=2, r=8), in_=stage[:].rearrange(split, h=2, r=8))
         permute_next()
-        bt_ps = psum.tile([P, 2, P], BF16, tag="bank7", name="bt_ps")
+        bt_ps = psum.tile([P, 3, P], BF16, tag="bank7", name="bt_ps")
         for h in range(2):
             nc.tensor.transpose(bt_ps[:, h, :], stage_p[:, 128 * h : 128 * (h + 1)], ident[:])
-        nc.vector.tensor_copy(
-            out=bias[:].rearrange("p (i h) -> p i h", h=2), in_=bt_ps[:, :, 0:16].rearrange("p h i -> p i h")
+        nc.tensor.matmul(
+            bt_ps[:, 2, 0:1],
+            lhsT=stage[:, 0:1].to_broadcast([P, P]),
+            rhs=ident[:, 16:17],
+            start=True,
+            stop=True,
         )
+        nc.vector.tensor_copy(
+            out=bias[:].rearrange("p (i h) -> p i h", h=2), in_=bt_ps[:, 0:2, 0:16].rearrange("p h i -> p i h")
+        )
+        nc.vector.tensor_copy(out=alpha_f[:], in_=bt_ps[:, 2, 0:1])
         acc_a += [psum.tile([P, 512], F32, tag="bank%d" % j, name="acc_a%d" % j) for j in range(4, 8)]
         low_a = PIECES.index((0, 7, 0, 4)) + 1
         low_b = PIECES.index((1, 7, 0, 4)) + 1
@@ -257,7 +268,6 @@ def tile_adaptivegraphconstruction_w_kernel(
         run(first_b, first_b + 4, acc_b, between=todo)
         acc_b += [psum.tile([P, 512], F32, tag="bank%d" % j, name="acc_b%d" % j) for j in range(4, 8)]
         run(first_b + 4, low_b, acc_b)
-        nc.vector.tensor_copy(out=alpha_f[:], in_=alpha_bf[:])
         close = PIECES.index((1, 7, 4, 2)) + 1
         run(low_b, close, acc_b, between=empty(1, acc_b, 0))
         evacuate(1, acc_b, 5, False)

@@ -27,7 +27,8 @@ PIECES = (
     + [(0, g, j, 4) for j in (0, 4) for g in range(4, 8)]
     + [(1, g, j, 4) for j in (0, 4) for g in range(4)]
     + [(1, g, 0, 4) for g in range(4, 8)]
-    + [(1, 4, 4, 4), (1, 5, 4, 2), (1, 6, 4, 2), (1, 7, 4, 2), (1, 5, 6, 2), (1, 6, 6, 2), (1, 7, 6, 1), (1, 7, 7, 1)]
+    + [(1, 4, 4, 4), (1, 5, 4, 2), (1, 6, 4, 2), (1, 7, 4, 2)]
+    + [(1, 5, 6, 2), (1, 6, 6, 1), (1, 7, 6, 1), (1, 6, 7, 1), (1, 7, 7, 1)]
 )
 
 def tile_adaptivegraphconstruction_w_kernel(
@@ -271,12 +272,13 @@ def tile_adaptivegraphconstruction_w_kernel(
         close = PIECES.index((1, 7, 4, 2)) + 1
         run(low_b, close, acc_b, between=empty(1, acc_b, 0))
         evacuate(1, acc_b, 5, False)
+        run(close, close + 1, acc_b)
         evacuate(1, acc_b, 4, True)
-        run(close, len(PIECES) - 1, acc_b)
-        quantise_q(1, 4, 6)
+        run(close + 1, len(PIECES) - 2, acc_b)
         evacuate(1, acc_b, 6, True)
-        run(len(PIECES) - 1, len(PIECES), acc_b)
+        run(len(PIECES) - 2, len(PIECES), acc_b)
         evacuate(1, acc_b, 7, True)
+        quantise_q(1, 4, 6)
         quantise_q(1, 6, 7)
         quantise_q(1, 7, 8)
         g_ps = psum.tile([P, V], F32, tag="bank0", name="g_ps")

@@ -49,6 +49,7 @@ def tile_adaptivegraphconstruction_w_kernel(
         ident = keep.tile([P, P], BF16, name="ident")
         bias = keep.tile([P, 32], F32, name="bias")
         a_sb = keep.tile([P, V], BF16, name="a_sb")
+        alpha_bf = keep.tile([P, 1], BF16, name="alpha_bf")
         alpha_f = keep.tile([P, 1], F32, name="alpha_f")
         warm_in = keep.tile([P, 1], F32, name="warm_in")
         warm_out = keep.tile([P, 1], F32, name="warm_out")
@@ -171,6 +172,8 @@ def tile_adaptivegraphconstruction_w_kernel(
         masks.make_identity(nc, ident[:])
         for b in range(1, 4):
             nc.gpsimd.memset(planes_raw[b][:].bitcast(I32), 0)
+        nc.scalar.dma_start(out=stage[0:8, :], in_=ba.rearrange("(i c) -> i c", c=256))
+        nc.scalar.dma_start(out=stage[8:16, :], in_=bb.rearrange("(i c) -> i c", c=256))
         nc.scalar.activation(out=warm_out[:], in_=warm_in[:], func=ACT.Tanh)
 
         state = {"loaded": 0, "permuted": 0}
@@ -181,13 +184,15 @@ def tile_adaptivegraphconstruction_w_kernel(
             m, g, j0, n = PIECES[i]
             if i == 0:
                 load_x(0)
-                load_w(0)
                 load_scales(0, 0)
+                load_w(0)
                 return
             if m == 0 and j0 == (2 if g == 0 else 4 if g < 4 else 0) and g < 7:
                 load_x(g + 1)
             if (m, g, j0) == (0, 2, 0):
                 load_scales(0, 1)
+            if (m, g, j0) == (0, 7, 0):
+                nc.sync.dma_start(out=alpha_bf[:], in_=alpha.partition_broadcast(P))
             if (m, g, j0) == (0, 5, 4):
                 load_scales(1, 0)
             if (m, g, j0) == (1, 1, 4):
@@ -195,10 +200,6 @@ def tile_adaptivegraphconstruction_w_kernel(
             load_w(i)
             if i == len(PIECES) - 1:
                 nc.sync.dma_start(out=a_sb[:], in_=A[0])
-            if i == 1:
-                nc.sync.dma_start(out=stage[0:8, :], in_=ba.rearrange("(i c) -> i c", c=256))
-                nc.sync.dma_start(out=stage[8:16, :], in_=bb.rearrange("(i c) -> i c", c=256))
-                nc.sync.dma_start(out=stage[16:17, 0:1], in_=alpha.unsqueeze(0))
 
         def permute_next():
             i = state["permuted"]
@@ -224,29 +225,17 @@ def tile_adaptivegraphconstruction_w_kernel(
 
         while state["loaded"] < 8:
             load_next()
-        regroup_x(0)
-        permute_w(0)
-        quantise_x(0)
-        permute_scales(0)
-        state["permuted"] = 1
+        permute_next()
         acc_a = [psum.tile([P, 512], F32, tag="bank%d" % j, name="acc_a%d" % j) for j in range(4)]
         run(0, 2, acc_a, 0)
         nc.vector.tensor_copy(out=stage_p[:].rearrange(joined, h=2, r=8), in_=stage[:].rearrange(split, h=2, r=8))
         permute_next()
-        bt_ps = psum.tile([P, 3, P], BF16, tag="bank7", name="bt_ps")
+        bt_ps = psum.tile([P, 2, P], BF16, tag="bank7", name="bt_ps")
         for h in range(2):
             nc.tensor.transpose(bt_ps[:, h, :], stage_p[:, 128 * h : 128 * (h + 1)], ident[:])
-        nc.tensor.matmul(
-            bt_ps[:, 2, 0:1],
-            lhsT=stage[:, 0:1].to_broadcast([P, P]),
-            rhs=ident[:, 16:17],
-            start=True,
-            stop=True,
-        )
         nc.vector.tensor_copy(
-            out=bias[:].rearrange("p (i h) -> p i h", h=2), in_=bt_ps[:, 0:2, 0:16].rearrange("p h i -> p i h")
+            out=bias[:].rearrange("p (i h) -> p i h", h=2), in_=bt_ps[:, :, 0:16].rearrange("p h i -> p i h")
         )
-        nc.vector.tensor_copy(out=alpha_f[:], in_=bt_ps[:, 2, 0:1])
         acc_a += [psum.tile([P, 512], F32, tag="bank%d" % j, name="acc_a%d" % j) for j in range(4, 8)]
         low_a = PIECES.index((0, 7, 0, 4)) + 1
         low_b = PIECES.index((1, 7, 0, 4)) + 1
@@ -269,6 +258,7 @@ def tile_adaptivegraphconstruction_w_kernel(
         run(first_b, first_b + 4, acc_b, between=todo)
         acc_b += [psum.tile([P, 512], F32, tag="bank%d" % j, name="acc_b%d" % j) for j in range(4, 8)]
         run(first_b + 4, low_b, acc_b)
+        nc.vector.tensor_copy(out=alpha_f[:], in_=alpha_bf[:])
         close = PIECES.index((1, 7, 4, 2)) + 1
         run(low_b, close, acc_b, between=empty(1, acc_b, 0))
         evacuate(1, acc_b, 5, False)

from contextlib import ExitStack

import concourse.masks as masks
import concourse.mybir as mybir

F32 = mybir.dt.float32
BF16 = mybir.dt.bfloat16
I32 = mybir.dt.int32
U8 = mybir.dt.uint8
FP8X4 = mybir.dt.float8_e4m3fn_x4
ACT = mybir.ActivationFunctionType
ALU = mybir.AluOpType
AX = mybir.AxisListType

P = 128
C = 4096
IC = 2048
T = 2
V = 128
TV = T * V
GROUPS = C // 512
FLOPS = 2 * 2 * IC * C * TV + 2 * V * V * IC * T

PIECES = (
    [(0, 0, 0, 2), (0, 0, 2, 2), (0, 0, 4, 4)]
    + [(0, g, j, 4) for g in range(1, 4) for j in (0, 4)]
    + [(0, g, j, 4) for j in (0, 4) for g in range(4, 8)]
    + [(1, g, j, 4) for j in (0, 4) for g in range(4)]
    + [(1, g, 0, 4) for g in range(4, 8)]
    + [(1, 4, 4, 4), (1, 5, 4, 2), (1, 6, 4, 2), (1, 7, 4, 2)]
    + [(1, 5, 6, 2), (1, 6, 6, 1), (1, 7, 6, 1), (1, 6, 7, 1), (1, 7, 7, 1)]
)

def tile_adaptivegraphconstruction_w_kernel(
    tc, x, Wa_words, Wa_scales, ba, Wb_words, Wb_scales, bb, A, alpha, out
):
    nc = tc.nc
    words = (Wa_words, Wb_words)
    scales = (Wa_scales, Wb_scales)
    with ExitStack() as ctx:
        keep = ctx.enter_context(tc.tile_pool(name="keep", bufs=1))
        raw_pool = ctx.enter_context(tc.tile_pool(name="raw", bufs=14))
        w_pool = ctx.enter_context(tc.tile_pool(name="w", bufs=8))
        psum = ctx.enter_context(tc.psum_pool(name="psum", bufs=1))
        ctx.enter_context(tc.manual_schedule())

        stage = keep.tile([P, 256], BF16, name="stage")
        stage_p = keep.tile([P, 256], BF16, name="stage_p")
        ident = keep.tile([P, P], BF16, name="ident")
        bias = keep.tile([P, 32], F32, name="bias")
        a_sb = keep.tile([P, V], BF16, name="a_sb")
        alpha_bf = keep.tile([P, 1], BF16, name="alpha_bf")
        alpha_f = keep.tile([P, 1], F32, name="alpha_f")
        warm_in = keep.tile([P, 1], F32, name="warm_in")
        warm_out = keep.tile([P, 1], F32, name="warm_out")
        planes_raw = [keep.tile([P, IC], U8, name="planes_raw%d" % b, align_bytes=64) for b in range(4)]
        planes = [keep.tile([P, IC], U8, name="planes%d" % b, align_bytes=64) for b in range(4)]
        x_raw = [keep.tile([P, 4 * TV], BF16, name="x_raw%d" % g) for g in range(GROUPS)]
        x_grp = [keep.tile([P, 4 * TV], BF16, name="x_grp%d" % g, align_bytes=64) for g in range(GROUPS)]
        x_codes = [keep.tile([P, TV], I32, name="x_codes%d" % g, align_bytes=64) for g in range(GROUPS)]
        x_scales = [keep.tile([P, TV], U8, name="x_scales%d" % g, align_bytes=64) for g in range(GROUPS)]
        q_grp = [keep.tile([P, 4096], BF16, name="q_grp%d" % m, align_bytes=64) for m in range(2)]
        q_codes = [keep.tile([P, 1024], I32, name="q_codes%d" % m, align_bytes=64) for m in range(2)]
        q_scales = [keep.tile([P, 1024], U8, name="q_scales%d" % m, align_bytes=64) for m in range(2)]
        w_raw = {}
        w = {}

        xv = x.rearrange("n (g p j) t v -> (n g) p (j t v)", p=P, j=4)

        def load_x(g):
            nc.sync.dma_start(out=x_raw[g][:], in_=xv[g])

        def load_w(i):
            m, g, j0, n = PIECES[i]
            src = words[m][g].rearrange("p n t -> p (n t)")[:, 1024 * j0 : 1024 * (j0 + n)]
            raw = raw_pool.tile([P, 1024], I32, name="raw", align_bytes=64)
            w_raw[i] = raw
            nc.sync.dma_start(out=raw[:, 0 : 256 * n], in_=src.bitcast(I32))

        def load_scales(wsel, b):
            for quad in (0, 2, 1, 3):
                nc.sync.dma_start(
                    out=planes_raw[2 * wsel + b][32 * quad : 32 * quad + 16, :].bitcast(I32),
                    in_=scales[wsel][4 * b : 4 * b + 4, 4 * quad : 4 * quad + 4, :].bitcast(I32),
                )

        split = "p (b h r) -> p h b r"
        joined = "p (h b r) -> p h b r"

        def permute_scales(b):
            nc.vector.tensor_copy(
                out=planes[b][:].bitcast(I32).rearrange(joined, h=2, r=2),
                in_=planes_raw[b][:].bitcast(I32).rearrange(split, h=2, r=2),
            )

        def permute_w(i):
            n = PIECES[i][3]
            tile = w_pool.tile([P, 1024], I32, name="w", align_bytes=64)
            w[i] = tile
            nc.vector.tensor_copy(
                out=tile[:, 0 : 256 * n].rearrange(joined, h=2, r=8),
                in_=w_raw[i][:, 0 : 256 * n].rearrange(split, h=2, r=8),
            )

        def regroup_x(g):
            dst = x_grp[g][:].rearrange("p (c i t) -> p c t i", i=4, t=4)
            src = x_raw[g][:].rearrange("p (t c i) -> p c t i", t=4, i=4)
            if g == 0:
                nc.vector.tensor_copy(out=dst, in_=src)
            else:
                nc.scalar.copy(out=dst, in_=src)

        def quantise_x(g):
            nc.vector.quantize_mx(out=x_codes[g][:].bitcast(FP8X4), scales=x_scales[g][:], in_=x_grp[g][:])

        def passes(i, acc):
            m, g, j0, n = PIECES[i]
            k = 4 * (g % 4)
            for j in range(j0, j0 + n):
                for u in range(2):
                    col = 1024 * u + 128 * j
                    at = 128 * n * u + 128 * (j - j0)
                    nc.tensor.matmul_mx(
                        out=acc[j][:, TV * u : TV * (u + 1)],
                        lhsT=w[i][:, at : at + 128].bitcast(FP8X4),
                        lhsT_scale=planes[2 * m + g // 4][k:P, col : col + 128],
                        rhs=x_codes[g][:].bitcast(FP8X4),
                        rhs_scale=x_scales[g][:],
                        start=(g == 0 and u == 0),
                        stop=(g == GROUPS - 1 and u == 1),
                    )

        def evacuate(m, acc, j, on_vector):
            dst = q_grp[m][:, 512 * j : 512 * (j + 1)].rearrange("p (v u t) -> p v u t", u=2, t=T)
            src = acc[j][:].rearrange("p (u t v) -> p v u t", u=2, t=T)
            row = 16 * m + 2 * j
            if on_vector:
                both = bias[:, row : row + 2].unsqueeze(1).unsqueeze(3).to_broadcast([P, V, 2, T])
                nc.vector.tensor_tensor(out=dst, in0=src, in1=both, op=ALU.add)
            else:
                for u in range(2):
                    nc.scalar.activation(
                        out=dst[:, :, u, :],
                        in_=src[:, :, u, :],
                        func=ACT.Identity,
                        bias=bias[:, row + u : row + u + 1],
                        scale=1.0,
                    )

        def quantise_q(m, j0, j1):
            nc.vector.quantize_mx(
                out=q_codes[m][:, 128 * j0 : 128 * j1].bitcast(FP8X4),
                scales=q_scales[m][:, 128 * j0 : 128 * j1],
                in_=q_grp[m][:, 512 * j0 : 512 * j1],
            )

        def second(g_ps, j):
            cols = slice(128 * j, 128 * (j + 1))
            nc.tensor.matmul_mx(
                out=g_ps[:],
                lhsT=q_codes[0][:, cols].bitcast(FP8X4),
                lhsT_scale=q_scales[0][:, cols],
                rhs=q_codes[1][:, cols].bitcast(FP8X4),
                rhs_scale=q_scales[1][:, cols],
                start=(j == 0),
                stop=(j == 7),
            )

        nc.vector.memset(planes_raw[0][:].bitcast(I32), 0)
        nc.vector.memset(stage[:], 0.0)
        nc.vector.memset(warm_in[:], 0.0)
        masks.make_identity(nc, ident[:])
        for b in range(1, 4):
            nc.gpsimd.memset(planes_raw[b][:].bitcast(I32), 0)
        nc.scalar.dma_start(out=stage[0:8, :], in_=ba.rearrange("(i c) -> i c", c=256))
        nc.scalar.dma_start(out=stage[8:16, :], in_=bb.rearrange("(i c) -> i c", c=256))
        nc.scalar.activation(out=warm_out[:], in_=warm_in[:], func=ACT.Tanh)

        state = {"loaded": 0, "permuted": 0}

        def load_next():
            i = state["loaded"]
            state["loaded"] += 1
            m, g, j0, n = PIECES[i]
            if i == 0:
                load_x(0)
                load_scales(0, 0)
                load_w(0)
                return
            if m == 0 and j0 == (2 if g == 0 else 4 if g < 4 else 0) and g < 7:
                load_x(g + 1)
            if (m, g, j0) == (0, 2, 0):
                load_scales(0, 1)
            if (m, g, j0) == (0, 7, 0):
                nc.sync.dma_start(out=alpha_bf[:], in_=alpha.partition_broadcast(P))
            if (m, g, j0) == (0, 5, 4):
                load_scales(1, 0)
            if (m, g, j0) == (1, 1, 4):
                load_scales(1, 1)
            load_w(i)
            if i == len(PIECES) - 1:
                nc.sync.dma_start(out=a_sb[:], in_=A[0])

        def permute_next():
            i = state["permuted"]
            state["permuted"] += 1
            m, g, j0, n = PIECES[i]
            if m == 0 and j0 == 0:
                regroup_x(g)
            if g % 4 == 0 and j0 == 0:
                permute_scales(2 * m + g // 4)
            if m == 0 and j0 == 0:
                quantise_x(g)
            permute_w(i)

        def run(first, last, acc, lead=2, between=()):
            for i in range(first, last):
                while state["loaded"] < min(i + 12, len(PIECES)):
                    load_next()
                while state["permuted"] < min(i + 1 + lead, len(PIECES)):
                    permute_next()
                passes(i, acc)
                if i - first < len(between):
                    between[i - first]()

        while state["loaded"] < 8:
            load_next()
        permute_next()
        acc_a = [psum.tile([P, 512], F32, tag="bank%d" % j, name="acc_a%d" % j) for j in range(4)]
        run(0, 2, acc_a, 0)
        nc.vector.tensor_copy(out=stage_p[:].rearrange(joined, h=2, r=8), in_=stage[:].rearrange(split, h=2, r=8))
        permute_next()
        bt_ps = psum.tile([P, 2, P], BF16, tag="bank7", name="bt_ps")
        for h in range(2):
            nc.tensor.transpose(bt_ps[:, h, :], stage_p[:, 128 * h : 128 * (h + 1)], ident[:])
        nc.vector.tensor_copy(
            out=bias[:].rearrange("p (i h) -> p i h", h=2), in_=bt_ps[:, :, 0:16].rearrange("p h i -> p i h")
        )
        acc_a += [psum.tile([P, 512], F32, tag="bank%d" % j, name="acc_a%d" % j) for j in range(4, 8)]
        low_a = PIECES.index((0, 7, 0, 4)) + 1
        low_b = PIECES.index((1, 7, 0, 4)) + 1
        first_b = PIECES.index((1, 0, 0, 4))

        def empty(m, acc, j0):
            evacuate(m, acc, j0, False)
            evacuate(m, acc, j0 + 2, False)
            return [
                lambda: evacuate(m, acc, j0 + 1, True),
                lambda: evacuate(m, acc, j0 + 3, True),
                lambda: quantise_q(m, j0, j0 + 4),
            ]

        run(2, low_a, acc_a)
        run(low_a, first_b, acc_a, between=empty(0, acc_a, 0))

        todo = empty(0, acc_a, 4)
        acc_b = [psum.tile([P, 512], F32, tag="bank%d" % j, name="acc_b%d" % j) for j in range(4)]
        run(first_b, first_b + 4, acc_b, between=todo)
        acc_b += [psum.tile([P, 512], F32, tag="bank%d" % j, name="acc_b%d" % j) for j in range(4, 8)]
        run(first_b + 4, low_b, acc_b)
        nc.vector.tensor_copy(out=alpha_f[:], in_=alpha_bf[:])
        close = PIECES.index((1, 7, 4, 2)) + 1
        run(low_b, close, acc_b, between=empty(1, acc_b, 0))
        evacuate(1, acc_b, 5, False)
        run(close, close + 1, acc_b)
        evacuate(1, acc_b, 4, True)
        run(close + 1, len(PIECES) - 2, acc_b)
        evacuate(1, acc_b, 6, True)
        run(len(PIECES) - 2, len(PIECES), acc_b)
        evacuate(1, acc_b, 7, True)
        quantise_q(1, 4, 6)
        quantise_q(1, 6, 7)
        quantise_q(1, 7, 8)
        g_ps = psum.tile([P, V], F32, tag="bank0", name="g_ps")
        for j in range(8):
            second(g_ps, j)

        th = keep.tile([P, V], F32, name="th")
        z = keep.tile([P, V], F32, name="z")
        e = keep.tile([P, V], F32, name="e")
        res = keep.tile([P, V], F32, name="res")
        negmax = keep.tile([P, 1], F32, name="negmax")
        total = keep.tile([P, 1], F32, name="total")
        recip = keep.tile([P, 1], F32, name="recip")
        nc.scalar.activation(out=th[:], in_=g_ps[:], func=ACT.Tanh, scale=1.0 / (IC * T))
        nc.vector.scalar_tensor_tensor(
            out=z[:], in0=th[:], scalar=alpha_f[:, 0:1], in1=a_sb[:], op0=ALU.mult, op1=ALU.add
        )
        nc.vector.tensor_reduce(out=negmax[:], in_=z[:], axis=AX.X, op=ALU.max, negate=True)
        nc.scalar.activation(out=e[:], in_=z[:], func=ACT.Exp, bias=negmax[:, 0:1], scale=1.0, accum_out=total[:])
        nc.vector.reciprocal(out=recip[:], in_=total[:])
        nc.vector.tensor_scalar(out=res[:], in0=e[:], scalar1=recip[:, 0:1], scalar2=None, op0=ALU.mult)
        nc.sync.dma_start(out=out[0], in_=res[:])
